import numpy as np
import ml_dtypes


def mxq(x, axis, fmt="e4m3"):
    dtype, down = {"e4m3": (ml_dtypes.float8_e4m3fn, 7), "e5m2": (ml_dtypes.float8_e5m2, 14)}[fmt]
    v = np.moveaxis(np.asarray(x, np.float32).astype(ml_dtypes.bfloat16).astype(np.float64), axis, -1)
    blocks = v.reshape(v.shape[:-1] + (-1, 32))
    amax = np.abs(blocks).max(-1, keepdims=True)
    byte = np.maximum(np.where(amax > 0, np.frexp(amax)[1] - 1 + 127, 0) - down, 1)
    scale = np.exp2(byte - 127.0)
    codes = (blocks / scale).astype(np.float32).astype(dtype).astype(np.float64)
    return np.moveaxis((codes * scale).reshape(v.shape), -1, axis)


WIDE = False


def mx_kscale(k):
    if not WIDE:
        return np.ones(k)
    levels = np.array([10, -10, 5, -5, 0])
    if k % 512:
        return np.exp2(np.random.permutation(np.resize(levels, k // 32))).repeat(32)
    a = np.empty((k // 512, 16))
    for p in range(k // 512):
        a[p, :8] = np.random.permutation(np.resize(levels, 8))
        for g in range(8):
            far = levels[np.abs(levels - a[p, g]) >= 10]
            a[p, g + 8] = far[np.random.randint(len(far))]
    return np.exp2(a.ravel()).repeat(32)


BF16 = ml_dtypes.bfloat16


def bf(x):
    return np.asarray(x, np.float32).astype(BF16)


def f64(x):
    return np.asarray(x).astype(np.float64)


S, H, E, P, C = 4096, 128, 416, 64, 32
IN0 = E + P + C + 4 * H


def sigmoid(v):
    return 1.0 / (1.0 + np.exp(-v))


def lstm_gates(g, c):
    i, f, gg, o = np.split(g, 4, axis=-1)
    c2 = sigmoid(f) * c + sigmoid(i) * np.tanh(gg)
    return sigmoid(o) * np.tanh(c2)


def setup_inputs():
    n = np.random.standard_normal
    s = mx_kscale(IN0)
    a1, a2, a3, a4 = 2 * H, 4 * H, 4 * H + E, 4 * H + E + P
    d = {"hn_chunks": bf(n((S, 2 * H)) * s[:a1]), "hn_tags": bf(n((S, 2 * H)) * s[a1:a2]), "x": bf(n((S, E)) * s[a2:a3]),
         "tags": bf(n((S, P)) * s[a3:a4]), "chunks": bf(n((S, C)) * s[a4:]),
         "h0": bf(n((2, S, H))), "c0": bf(n((2, S, H)))}
    for k in ("f", "b"):
        d["wih_" + k] = bf(n((4 * H, IN0)) / np.sqrt(IN0) / s)
        d["whh_" + k] = bf(n((4 * H, H)) * 0.7 / np.sqrt(H))
        d["bih_" + k] = bf(n(4 * H) * 0.2)
        d["bhh_" + k] = bf(n(4 * H) * 0.2)
    return d


def reference(hn_chunks, hn_tags, x, tags, chunks, h0, c0, wih_f, whh_f, bih_f, bhh_f, wih_b, whh_b, bih_b, bhh_b):
    gt = np.concatenate([f64(hn_chunks), f64(hn_tags), f64(x), f64(tags), f64(chunks)], axis=1)
    gq = mxq(gt, 1, "e4m3")
    gf = (gq @ mxq(f64(wih_f), 1, "e4m3").T) + f64(bih_f) + f64(h0)[0] @ f64(whh_f).T + f64(bhh_f)
    gb = (gq @ mxq(f64(wih_b), 1, "e4m3").T) + f64(bih_b) + f64(h0)[1] @ f64(whh_b).T + f64(bhh_b)
    return np.concatenate([lstm_gates(gf, f64(c0)[0]), lstm_gates(gb, f64(c0)[1])], axis=-1)

@@ -1,0 +1,333 @@
+from contextlib import ExitStack
+
+import concourse.mybir as mybir
+from concourse.masks import make_identity
+
+F32 = mybir.dt.float32
+BF16 = mybir.dt.bfloat16
+U32 = mybir.dt.uint32
+U8 = mybir.dt.uint8
+FP8X4 = mybir.dt.float8_e4m3fn_x4
+ACT = mybir.ActivationFunctionType
+ALU = mybir.AluOpType
+
+P = 128
+S = 4096
+H = 128
+IN0 = 1024
+DIRS = 2
+GATES = 4 * H
+PACK = 4
+PAIR = 2
+HALVES = PACK // PAIR
+PASSES = IN0 // (P * PACK)
+TILES = S // P
+ROUND = 2
+ROUNDS = TILES // ROUND
+LOAD_TILES = 4
+LOADS = TILES // LOAD_TILES
+LOAD_ROUNDS = LOAD_TILES // ROUND
+LOADS_AHEAD = 3
+VECTOR_ROUNDS = 1
+
+FLOPS = 2 * S * (IN0 + H) * DIRS * GATES
+
+
+def flip_words(nc, banks, row_words, identity):
+    pass_words = HALVES * P
+    flipped = banks.tile([P, PASSES, HALVES, P], F32)
+    for g in range(PASSES):
+        for u in range(HALVES):
+            words = slice(g * pass_words + u, (g + 1) * pass_words, HALVES)
+            nc.tensor.transpose(flipped[:, g, u, :], row_words[:, words], identity)
+    return flipped[:].rearrange("p g u r -> p g r u")
+
+
+def tile_dependency_pa_t_kernel(
+    tc, hn_chunks, hn_tags, x, tags, chunks, h0, c0,
+    wih_f, whh_f, bih_f, bhh_f, wih_b, whh_b, bih_b, bhh_b, out,
+):
+    nc = tc.nc
+    wih = [wih_f, wih_b]
+    whh = [whh_f, whh_b]
+    bih = [bih_f, bih_b]
+    bhh = [bhh_f, bhh_b]
+
+    with ExitStack() as ctx:
+        ctx.enter_context(tc.manual_schedule())
+        keep = ctx.enter_context(tc.tile_pool(name="keep", bufs=1))
+        double = ctx.enter_context(tc.tile_pool(name="double", bufs=2))
+        triple = ctx.enter_context(tc.tile_pool(name="triple", bufs=3))
+        gate_pool = ctx.enter_context(tc.tile_pool(name="gate_pool", bufs=4))
+        flip_banks = ctx.enter_context(tc.psum_pool(name="flip_banks", bufs=2))
+        state_banks = ctx.enter_context(tc.psum_pool(name="state_banks", bufs=1))
+        plain_banks = ctx.enter_context(tc.psum_pool(name="plain_banks", bufs=2))
+        mx_banks = ctx.enter_context(tc.psum_pool(name="mx_banks", bufs=3))
+
+        identity_bf16 = keep.tile([P, P], BF16)
+        make_identity(nc, identity_bf16[:])
+        identity_f32 = keep.tile([P, P], F32)
+        make_identity(nc, identity_f32[:])
+        ones = keep.tile([P, P], BF16)
+        nc.vector.memset(ones[:], 1.0)
+        bias_rows = keep.tile([P, DIRS, GATES], BF16)
+        nc.vector.memset(bias_rows[:], 0.0)
+        warm = keep.tile([P, 1], F32)
+        nc.vector.memset(warm[:], 0.0)
+        nc.scalar.activation(out=warm[:], in_=warm[:], func=ACT.Sigmoid)
+
+        whh_rows = keep.tile([P, DIRS, 4, H], BF16)
+        wih_rows = keep.tile([P, DIRS * 4 * IN0], BF16)
+        gt = keep.tile([P, TILES * IN0], BF16)
+        h0_rows = keep.tile([P, DIRS, TILES, H], BF16)
+        c0_rows = keep.tile([P, DIRS, TILES, H], BF16)
+
+        wih_features = wih_rows[:].rearrange("p (d r k) -> p d r k", d=DIRS, k=IN0)
+        wih_words = wih_rows[:].bitcast(F32).rearrange("p (d r w) -> p d r w", d=DIRS, w=IN0 // PAIR)
+        gt_features = gt[:].rearrange("p (t k) -> p t k", k=IN0)
+        gt_words = gt[:].bitcast(F32).rearrange("p (t w) -> p t w", w=IN0 // PAIR)
+
+        def load_weights(d):
+            for rows in (slice(0, 2), slice(2, 4)):
+                nc.sync.dma_start(
+                    out=wih_features[:, d, rows, :],
+                    in_=wih[d].rearrange("(r p) k -> p r k", p=P)[:, rows, :],
+                )
+
+        def load_state(rows, state, load):
+            tiles = slice(load * LOAD_TILES, (load + 1) * LOAD_TILES)
+            nc.sync.dma_start(
+                out=rows[:, :, tiles, :],
+                in_=state.rearrange("d (p t) h -> p d t h", t=TILES)[:, :, tiles, :],
+            )
+
+        def load_features(load):
+            tiles = slice(load * LOAD_TILES, (load + 1) * LOAD_TILES)
+            first = 0
+            for stream in (hn_chunks, hn_tags, x, tags, chunks):
+                width = stream.shape[1]
+                nc.sync.dma_start(
+                    out=gt_features[:, tiles, first : first + width],
+                    in_=stream.rearrange("(p t) c -> p t c", t=TILES)[:, tiles, :],
+                )
+                first += width
+
+        for d in range(DIRS):
+            nc.sync.dma_start(out=whh_rows[:, d], in_=whh[d].rearrange("(r p) h -> p r h", p=P))
+            nc.sync.dma_start(out=bias_rows[0:1, d, :], in_=bih[d].rearrange("(o n) -> o n", o=1))
+            nc.sync.dma_start(out=bias_rows[1:2, d, :], in_=bhh[d].rearrange("(o n) -> o n", o=1))
+        load_state(h0_rows, h0, 0)
+        load_weights(0)
+        load_features(0)
+        load_weights(1)
+
+        def load_tokens(load):
+            load_state(h0_rows, h0, load)
+            load_features(load)
+            load_state(c0_rows, c0, load)
+
+        load_state(h0_rows, h0, 1)
+        load_features(1)
+        load_state(c0_rows, c0, 0)
+        load_state(c0_rows, c0, 1)
+        for load in range(2, LOADS_AHEAD):
+            load_tokens(load)
+
+        whh_t = keep.tile([P, DIRS, 4, H], BF16)
+        bias = keep.tile([P, DIRS, GATES], F32)
+        wih_codes = keep.tile([P, PASSES, DIRS, GATES], U32, align_bytes=64)
+        wih_scales = keep.tile([P, PASSES, DIRS, GATES], U8, align_bytes=64)
+        state_bank_of = {}
+        flipped_of = {}
+        h0_t_of = {}
+        grouped_of = {}
+        operand_of = {}
+        gates_of = {}
+        out_gate_of = {}
+        cell_of = {}
+        cell_tanh_of = {}
+        blocks = [(d, a) for d in range(DIRS) for a in range(ROUND)]
+
+        def prepare_small_weights(d):
+            state_bank = state_banks.tile([P, 4, P], BF16)
+            for r in range(4):
+                nc.tensor.transpose(state_bank[:, r, :], whh_rows[:, d, r, :], identity_bf16[:])
+            nc.scalar.copy(out=whh_t[:, d], in_=state_bank[:])
+            plain_bank = plain_banks.tile([P, GATES], F32)
+            nc.tensor.matmul(out=plain_bank[:], lhsT=ones[:], rhs=bias_rows[:, d, :], start=True, stop=True)
+            nc.vector.tensor_copy(out=bias[:, d, :], in_=plain_bank[:])
+
+        def prepare_weights(d):
+            wih_grouped = keep.tile([P, PASSES * GATES * PACK], BF16, align_bytes=64)
+            wih_grouped_words = wih_grouped[:].bitcast(F32).rearrange(
+                "p (g n u) -> p g n u", g=PASSES, u=HALVES
+            )
+            for r in range(4):
+                flipped = flip_words(nc, flip_banks, wih_words[:, d, r, :], identity_f32[:])
+                if r % 2 == 0:
+                    nc.scalar.copy(out=wih_grouped_words[:, :, r * P : (r + 1) * P, :], in_=flipped)
+                else:
+                    nc.vector.tensor_copy(out=wih_grouped_words[:, :, r * P : (r + 1) * P, :], in_=flipped)
+            for g in range(PASSES):
+                nc.vector.quantize_mx(
+                    out=wih_codes[:, g, d, :].bitcast(FP8X4),
+                    scales=wih_scales[:, g, d, :],
+                    in_=wih_grouped[:].rearrange("p (g c) -> p g c", g=PASSES)[:, g, :],
+                )
+
+        def flip_state(r):
+            state_bank = state_banks.tile([P, DIRS, ROUND, P], BF16)
+            for d in range(DIRS):
+                for a in range(ROUND):
+                    nc.tensor.transpose(
+                        state_bank[:, d, a, :], h0_rows[:, d, r * ROUND + a, :], identity_bf16[:]
+                    )
+            state_bank_of[r] = state_bank
+
+        def collect_state(r):
+            h0_t = triple.tile([P, DIRS, ROUND, P], BF16)
+            nc.scalar.copy(out=h0_t[:], in_=state_bank_of[r][:])
+            h0_t_of[r] = h0_t
+
+        def flip_features(r):
+            flipped_of[r] = [
+                flip_words(nc, flip_banks, gt_words[:, r * ROUND + a, :], identity_f32[:])
+                for a in range(ROUND)
+            ]
+
+        def collect_features(r):
+            grouped = double.tile([P, ROUND * PASSES * P * PACK], BF16, align_bytes=64)
+            grouped_words = grouped[:].bitcast(F32).rearrange(
+                "p (a g r u) -> p a g r u", a=ROUND, g=PASSES, u=HALVES
+            )
+            for a in range(ROUND):
+                nc.scalar.copy(out=grouped_words[:, a], in_=flipped_of[r][a])
+            grouped_of[r] = grouped
+
+        def quantise_features(r):
+            codes = triple.tile([P, ROUND, PASSES, P], U32, align_bytes=64)
+            scales = triple.tile([P, ROUND, PASSES, P], U8, align_bytes=64)
+            nc.vector.quantize_mx(
+                out=codes[:].rearrange("p a g r -> p (a g r)").bitcast(FP8X4),
+                scales=scales[:].rearrange("p a g r -> p (a g r)"),
+                in_=grouped_of[r][:],
+            )
+            operand_of[r] = (codes, scales)
+
+        def recurrent_term(r, d, a):
+            if (d, a) == blocks[0]:
+                gates = gate_pool.tile([P, DIRS, ROUND, GATES], F32)
+                gates_of[r] = gates
+            bias_on_tensor = (d, a) == blocks[-1]
+            plain_bank = plain_banks.tile([P, GATES], F32)
+            nc.tensor.matmul(
+                out=plain_bank[:],
+                lhsT=h0_t_of[r][:, d, a, :],
+                rhs=whh_t[:, d].rearrange("p r h -> p (r h)"),
+                start=True,
+                stop=not bias_on_tensor,
+            )
+            if bias_on_tensor:
+                nc.tensor.matmul(
+                    out=plain_bank[:], lhsT=ones[:], rhs=bias_rows[:, d, :], start=False, stop=True
+                )
+                nc.scalar.copy(out=gates_of[r][:, d, a, :], in_=plain_bank[:])
+            else:
+                nc.vector.tensor_tensor(
+                    out=gates_of[r][:, d, a, :], in0=plain_bank[:], in1=bias[:, d, :], op=ALU.add
+                )
+
+        def input_term(r, d, a):
+            codes, scales = operand_of[r]
+            mx_bank = mx_banks.tile([P, GATES], F32)
+            for g in range(PASSES):
+                nc.tensor.matmul_mx(
+                    out=mx_bank[:],
+                    lhsT=codes[:, a, g, :].bitcast(FP8X4),
+                    lhsT_scale=scales[:, a, g, :],
+                    rhs=wih_codes[:, g, d, :].bitcast(FP8X4),
+                    rhs_scale=wih_scales[:, g, d, :],
+                    start=(g == 0),
+                    stop=(g == PASSES - 1),
+                )
+            nc.vector.tensor_tensor(
+                out=gates_of[r][:, d, a, :], in0=mx_bank[:], in1=gates_of[r][:, d, a, :], op=ALU.add
+            )
+
+        def new_cell(r):
+            gates = gates_of[r]
+            tiles = slice(r * ROUND, (r + 1) * ROUND)
+            nc.scalar.activation(out=gates[:, :, :, 0 : 2 * H], in_=gates[:, :, :, 0 : 2 * H], func=ACT.Sigmoid)
+            nc.scalar.activation(out=gates[:, :, :, 2 * H : 3 * H], in_=gates[:, :, :, 2 * H : 3 * H], func=ACT.Tanh)
+            out_gate = triple.tile([P, DIRS, ROUND, H], F32)
+            nc.scalar.activation(out=out_gate[:], in_=gates[:, :, :, 3 * H : 4 * H], func=ACT.Sigmoid)
+            out_gate_of[r] = out_gate
+            engine = nc.vector if r >= ROUNDS - VECTOR_ROUNDS else nc.gpsimd
+            kept = double.tile([P, DIRS, ROUND, H], F32)
+            engine.tensor_tensor(
+                out=kept[:], in0=gates[:, :, :, H : 2 * H], in1=c0_rows[:, :, tiles, :], op=ALU.mult
+            )
+            written = double.tile([P, DIRS, ROUND, H], F32)
+            engine.tensor_tensor(
+                out=written[:], in0=gates[:, :, :, 0:H], in1=gates[:, :, :, 2 * H : 3 * H], op=ALU.mult
+            )
+            cell = triple.tile([P, DIRS, ROUND, H], F32)
+            engine.tensor_tensor(out=cell[:], in0=kept[:], in1=written[:], op=ALU.add)
+            cell_of[r] = cell
+
+        def squash_cell(r):
+            cell_tanh = double.tile([P, DIRS, ROUND, H], F32)
+            nc.scalar.activation(out=cell_tanh[:], in_=cell_of[r][:], func=ACT.Tanh)
+            cell_tanh_of[r] = cell_tanh
+
+        def new_hidden(r):
+            tiles = slice(r * ROUND, (r + 1) * ROUND)
+            hidden = triple.tile([P, ROUND, DIRS, H], F32)
+            nc.vector.tensor_tensor(
+                out=hidden[:].rearrange("p a d h -> p d a h"),
+                in0=out_gate_of[r][:],
+                in1=cell_tanh_of[r][:],
+                op=ALU.mult,
+            )
+            nc.sync.dma_start(
+                out=out.rearrange("(p t) (d h) -> p t d h", t=TILES, d=DIRS)[:, tiles, :, :],
+                in_=hidden[:],
+            )
+
+        for d in range(DIRS):
+            prepare_small_weights(d)
+        for r in range(2):
+            flip_state(r)
+            collect_state(r)
+        for d, a in blocks:
+            recurrent_term(0, d, a)
+        prepare_weights(0)
+        for r in range(2):
+            flip_features(r)
+            collect_features(r)
+            quantise_features(r)
+        prepare_weights(1)
+
+        for i in range(ROUNDS + 2):
+            load = i // LOAD_ROUNDS + LOADS_AHEAD
+            if i % LOAD_ROUNDS == 0 and load < LOADS:
+                load_tokens(load)
+            if 1 <= i <= ROUNDS:
+                new_cell(i - 1)
+            if i >= 2:
+                squash_cell(i - 2)
+            for d in range(DIRS):
+                for a in range(ROUND):
+                    if i < ROUNDS:
+                        input_term(i, d, a)
+                    if i + 1 < ROUNDS:
+                        recurrent_term(i + 1, d, a)
+                if d == 0 and i + 2 < ROUNDS:
+                    flip_features(i + 2)
+                    flip_state(i + 2)
+                    collect_features(i + 2)
+                    collect_state(i + 2)
+            if i >= 2:
+                new_hidden(i - 2)
+            if i + 2 < ROUNDS:
+                quantise_features(i + 2)

@@ -24,23 +24,26 @@ PASSES = IN0 // (P * PACK)
 TILES = S // P
 ROUND = 2
 ROUNDS = TILES // ROUND
-LOAD_TILES = 4
-LOADS = TILES // LOAD_TILES
-LOAD_ROUNDS = LOAD_TILES // ROUND
-LOADS_AHEAD = 3
-VECTOR_ROUNDS = 1
+UNITS = ROUNDS * DIRS
+STREAM_LOADS = 8
+LOADS_AHEAD = 5
+LAG = 3
+HOLD = 2
+LEAD = 2
+WARM_MATMULS = 6
+VECTOR_UNITS = 2
 
 FLOPS = 2 * S * (IN0 + H) * DIRS * GATES
 
 
 def flip_words(nc, banks, row_words, identity):
     pass_words = HALVES * P
-    flipped = banks.tile([P, PASSES, HALVES, P], F32)
+    bank = banks.tile([P, PASSES, HALVES, P], F32)
     for g in range(PASSES):
         for u in range(HALVES):
             words = slice(g * pass_words + u, (g + 1) * pass_words, HALVES)
-            nc.tensor.transpose(flipped[:, g, u, :], row_words[:, words], identity)
-    return flipped[:].rearrange("p g u r -> p g r u")
+            nc.tensor.transpose(bank[:, g, u, :], row_words[:, words], identity)
+    return bank[:].rearrange("p g u r -> p g r u")
 
 
 def tile_dependency_pa_t_kernel(
@@ -56,19 +59,18 @@ def tile_dependency_pa_t_kernel(
     with ExitStack() as ctx:
         ctx.enter_context(tc.manual_schedule())
         keep = ctx.enter_context(tc.tile_pool(name="keep", bufs=1))
-        double = ctx.enter_context(tc.tile_pool(name="double", bufs=2))
-        triple = ctx.enter_context(tc.tile_pool(name="triple", bufs=3))
-        gate_pool = ctx.enter_context(tc.tile_pool(name="gate_pool", bufs=4))
-        flip_banks = ctx.enter_context(tc.psum_pool(name="flip_banks", bufs=2))
-        state_banks = ctx.enter_context(tc.psum_pool(name="state_banks", bufs=1))
-        plain_banks = ctx.enter_context(tc.psum_pool(name="plain_banks", bufs=2))
-        mx_banks = ctx.enter_context(tc.psum_pool(name="mx_banks", bufs=3))
+        double = ctx.enter_context(tc.tile_pool(name="double", bufs=4))
+        triple = ctx.enter_context(tc.tile_pool(name="triple", bufs=8))
+        stream = ctx.enter_context(tc.tile_pool(name="stream", bufs=STREAM_LOADS))
+        state_pool = ctx.enter_context(tc.tile_pool(name="state_pool", bufs=LEAD + 3))
+        gate_pool = ctx.enter_context(tc.tile_pool(name="gate_pool", bufs=2 * LEAD + 5))
+        banks = ctx.enter_context(tc.psum_pool(name="banks", bufs=8))
 
         identity_bf16 = keep.tile([P, P], BF16)
         make_identity(nc, identity_bf16[:])
         identity_f32 = keep.tile([P, P], F32)
         make_identity(nc, identity_f32[:])
-        ones = keep.tile([P, P], BF16)
+        ones = keep.tile([P, GATES], BF16)
         nc.vector.memset(ones[:], 1.0)
         bias_rows = keep.tile([P, DIRS, GATES], BF16)
         nc.vector.memset(bias_rows[:], 0.0)
@@ -78,14 +80,11 @@ def tile_dependency_pa_t_kernel(
 
         whh_rows = keep.tile([P, DIRS, 4, H], BF16)
         wih_rows = keep.tile([P, DIRS * 4 * IN0], BF16)
-        gt = keep.tile([P, TILES * IN0], BF16)
         h0_rows = keep.tile([P, DIRS, TILES, H], BF16)
         c0_rows = keep.tile([P, DIRS, TILES, H], BF16)
 
         wih_features = wih_rows[:].rearrange("p (d r k) -> p d r k", d=DIRS, k=IN0)
         wih_words = wih_rows[:].bitcast(F32).rearrange("p (d r w) -> p d r w", d=DIRS, w=IN0 // PAIR)
-        gt_features = gt[:].rearrange("p (t k) -> p t k", k=IN0)
-        gt_words = gt[:].bitcast(F32).rearrange("p (t w) -> p t w", w=IN0 // PAIR)
 
         def load_weights(d):
             for rows in (slice(0, 2), slice(2, 4)):
@@ -94,44 +93,47 @@ def tile_dependency_pa_t_kernel(
                     in_=wih[d].rearrange("(r p) k -> p r k", p=P)[:, rows, :],
                 )
 
-        def load_state(rows, state, load):
-            tiles = slice(load * LOAD_TILES, (load + 1) * LOAD_TILES)
+        def load_state(rows, state, first, last):
             nc.sync.dma_start(
-                out=rows[:, :, tiles, :],
-                in_=state.rearrange("d (p t) h -> p d t h", t=TILES)[:, :, tiles, :],
+                out=rows[:, :, first:last, :],
+                in_=state.rearrange("d (p t) h -> p d t h", t=TILES)[:, :, first:last, :],
             )
 
-        def load_features(load):
-            tiles = slice(load * LOAD_TILES, (load + 1) * LOAD_TILES)
+        gt_of = {}
+
+        def load_features(r):
+            gt = stream.tile([P, ROUND * IN0], BF16)
+            gt_features = gt[:].rearrange("p (a k) -> p a k", k=IN0)
+            tiles = slice(r * ROUND, (r + 1) * ROUND)
             first = 0
-            for stream in (hn_chunks, hn_tags, x, tags, chunks):
-                width = stream.shape[1]
+            for features in (hn_chunks, hn_tags, x, tags, chunks):
+                width = features.shape[1]
                 nc.sync.dma_start(
-                    out=gt_features[:, tiles, first : first + width],
-                    in_=stream.rearrange("(p t) c -> p t c", t=TILES)[:, tiles, :],
+                    out=gt_features[:, :, first : first + width],
+                    in_=features.rearrange("(p t) c -> p t c", t=TILES)[:, tiles, :],
                 )
                 first += width
+            gt_of[r] = gt[:].bitcast(F32).rearrange("p (a w) -> p a w", w=IN0 // PAIR)
 
-        for d in range(DIRS):
+        def load_small_weights(d):
             nc.sync.dma_start(out=whh_rows[:, d], in_=whh[d].rearrange("(r p) h -> p r h", p=P))
             nc.sync.dma_start(out=bias_rows[0:1, d, :], in_=bih[d].rearrange("(o n) -> o n", o=1))
             nc.sync.dma_start(out=bias_rows[1:2, d, :], in_=bhh[d].rearrange("(o n) -> o n", o=1))
-        load_state(h0_rows, h0, 0)
+
+        load_small_weights(0)
+        load_state(h0_rows, h0, 0, 4)
         load_weights(0)
         load_features(0)
-        load_weights(1)
-
-        def load_tokens(load):
-            load_state(h0_rows, h0, load)
-            load_features(load)
-            load_state(c0_rows, c0, load)
-
-        load_state(h0_rows, h0, 1)
+        load_small_weights(1)
+        load_state(h0_rows, h0, 4, 8)
         load_features(1)
-        load_state(c0_rows, c0, 0)
-        load_state(c0_rows, c0, 1)
-        for load in range(2, LOADS_AHEAD):
-            load_tokens(load)
+        load_weights(1)
+        load_features(2)
+        load_state(c0_rows, c0, 0, 8)
+        load_state(h0_rows, h0, 8, 20)
+        for r in range(3, LOADS_AHEAD):
+            load_features(r)
+        load_state(c0_rows, c0, 8, 20)
 
         whh_t = keep.tile([P, DIRS, 4, H], BF16)
         bias = keep.tile([P, DIRS, GATES], F32)
@@ -146,63 +148,61 @@ def tile_dependency_pa_t_kernel(
         out_gate_of = {}
         cell_of = {}
         cell_tanh_of = {}
-        blocks = [(d, a) for d in range(DIRS) for a in range(ROUND)]
 
         def prepare_small_weights(d):
-            state_bank = state_banks.tile([P, 4, P], BF16)
+            bank = banks.tile([P, 4, P], BF16)
             for r in range(4):
-                nc.tensor.transpose(state_bank[:, r, :], whh_rows[:, d, r, :], identity_bf16[:])
-            nc.scalar.copy(out=whh_t[:, d], in_=state_bank[:])
-            plain_bank = plain_banks.tile([P, GATES], F32)
-            nc.tensor.matmul(out=plain_bank[:], lhsT=ones[:], rhs=bias_rows[:, d, :], start=True, stop=True)
-            nc.vector.tensor_copy(out=bias[:, d, :], in_=plain_bank[:])
+                nc.tensor.transpose(bank[:, r, :], whh_rows[:, d, r, :], identity_bf16[:])
+            nc.scalar.copy(out=whh_t[:, d], in_=bank[:])
+            bank = banks.tile([P, GATES], F32)
+            nc.tensor.matmul(out=bank[:], lhsT=ones[:, 0:P], rhs=bias_rows[:, d, :], start=True, stop=True)
+            nc.scalar.copy(out=bias[:, d, :], in_=bank[:])
 
-        def prepare_weights(d):
-            wih_grouped = keep.tile([P, PASSES * GATES * PACK], BF16, align_bytes=64)
-            wih_grouped_words = wih_grouped[:].bitcast(F32).rearrange(
+        wih_grouped_of = {}
+
+        def flip_weights(d, q):
+            if q == 0:
+                wih_grouped = keep.tile([P, PASSES * GATES * PACK], BF16, align_bytes=64)
+                wih_grouped_of[d] = wih_grouped
+            wih_grouped_words = wih_grouped_of[d][:].bitcast(F32).rearrange(
                 "p (g n u) -> p g n u", g=PASSES, u=HALVES
             )
-            for r in range(4):
-                flipped = flip_words(nc, flip_banks, wih_words[:, d, r, :], identity_f32[:])
-                if r % 2 == 0:
-                    nc.scalar.copy(out=wih_grouped_words[:, :, r * P : (r + 1) * P, :], in_=flipped)
-                else:
-                    nc.vector.tensor_copy(out=wih_grouped_words[:, :, r * P : (r + 1) * P, :], in_=flipped)
+            flipped = flip_words(nc, banks, wih_words[:, d, q, :], identity_f32[:])
+            nc.scalar.copy(out=wih_grouped_words[:, :, q * P : (q + 1) * P, :], in_=flipped)
+
+        def quantise_weights(d):
             for g in range(PASSES):
                 nc.vector.quantize_mx(
                     out=wih_codes[:, g, d, :].bitcast(FP8X4),
                     scales=wih_scales[:, g, d, :],
-                    in_=wih_grouped[:].rearrange("p (g c) -> p g c", g=PASSES)[:, g, :],
+                    in_=wih_grouped_of[d][:].rearrange("p (g c) -> p g c", g=PASSES)[:, g, :],
                 )
 
         def flip_state(r):
-            state_bank = state_banks.tile([P, DIRS, ROUND, P], BF16)
+            bank = banks.tile([P, DIRS, ROUND, P], BF16)
             for d in range(DIRS):
                 for a in range(ROUND):
                     nc.tensor.transpose(
-                        state_bank[:, d, a, :], h0_rows[:, d, r * ROUND + a, :], identity_bf16[:]
+                        bank[:, d, a, :], h0_rows[:, d, r * ROUND + a, :], identity_bf16[:]
                     )
-            state_bank_of[r] = state_bank
+            state_bank_of[r] = bank
 
         def collect_state(r):
-            h0_t = triple.tile([P, DIRS, ROUND, P], BF16)
+            h0_t = state_pool.tile([P, DIRS, ROUND, P], BF16)
             nc.scalar.copy(out=h0_t[:], in_=state_bank_of[r][:])
             h0_t_of[r] = h0_t
 
-        def flip_features(r):
-            flipped_of[r] = [
-                flip_words(nc, flip_banks, gt_words[:, r * ROUND + a, :], identity_f32[:])
-                for a in range(ROUND)
-            ]
+        def flip_features(r, a):
+            flipped_of[r, a] = flip_words(nc, banks, gt_of[r][:, a, :], identity_f32[:])
 
-        def collect_features(r):
-            grouped = double.tile([P, ROUND * PASSES * P * PACK], BF16, align_bytes=64)
-            grouped_words = grouped[:].bitcast(F32).rearrange(
+        def collect_features(r, a):
+            if a == 0:
+                grouped = double.tile([P, ROUND * PASSES * P * PACK], BF16, align_bytes=64)
+                grouped_of[r] = grouped
+            grouped_words = grouped_of[r][:].bitcast(F32).rearrange(
                 "p (a g r u) -> p a g r u", a=ROUND, g=PASSES, u=HALVES
             )
-            for a in range(ROUND):
-                nc.scalar.copy(out=grouped_words[:, a], in_=flipped_of[r][a])
-            grouped_of[r] = grouped
+            nc.scalar.copy(out=grouped_words[:, a], in_=flipped_of[r, a])
 
         def quantise_features(r):
             codes = triple.tile([P, ROUND, PASSES, P], U32, align_bytes=64)
@@ -214,35 +214,43 @@ def tile_dependency_pa_t_kernel(
             )
             operand_of[r] = (codes, scales)
 
-        def recurrent_term(r, d, a):
-            if (d, a) == blocks[0]:
-                gates = gate_pool.tile([P, DIRS, ROUND, GATES], F32)
-                gates_of[r] = gates
-            bias_on_tensor = (d, a) == blocks[-1]
-            plain_bank = plain_banks.tile([P, GATES], F32)
+        units = [(r, d) for d in range(DIRS) for r in range(2)]
+        units += [(r, d) for r in range(2, ROUNDS) for d in range(DIRS)]
+        terms = [(unit, a) for unit in range(UNITS) for a in range(ROUND)]
+
+        def recurrent_term(index, on_scalar):
+            if index >= len(terms):
+                return
+            unit, a = terms[index]
+            r, d = units[unit]
+            if a == 0:
+                gates = gate_pool.tile([P, ROUND, GATES], F32)
+                gates_of[unit] = gates
+            bank = banks.tile([P, GATES], F32)
             nc.tensor.matmul(
-                out=plain_bank[:],
+                out=bank[:],
                 lhsT=h0_t_of[r][:, d, a, :],
                 rhs=whh_t[:, d].rearrange("p r h -> p (r h)"),
                 start=True,
-                stop=not bias_on_tensor,
+                stop=not on_scalar,
             )
-            if bias_on_tensor:
+            if on_scalar:
                 nc.tensor.matmul(
-                    out=plain_bank[:], lhsT=ones[:], rhs=bias_rows[:, d, :], start=False, stop=True
+                    out=bank[:], lhsT=ones[:, 0:P], rhs=bias_rows[:, d, :], start=False, stop=True
                 )
-                nc.scalar.copy(out=gates_of[r][:, d, a, :], in_=plain_bank[:])
+                nc.scalar.copy(out=gates_of[unit][:, a, :], in_=bank[:])
             else:
                 nc.vector.tensor_tensor(
-                    out=gates_of[r][:, d, a, :], in0=plain_bank[:], in1=bias[:, d, :], op=ALU.add
+                    out=gates_of[unit][:, a, :], in0=bank[:], in1=bias[:, d, :], op=ALU.add
                 )
 
-        def input_term(r, d, a):
+        def input_term(unit, a):
+            r, d = units[unit]
             codes, scales = operand_of[r]
-            mx_bank = mx_banks.tile([P, GATES], F32)
+            bank = banks.tile([P, GATES], F32)
             for g in range(PASSES):
                 nc.tensor.matmul_mx(
-                    out=mx_bank[:],
+                    out=bank[:],
                     lhsT=codes[:, a, g, :].bitcast(FP8X4),
                     lhsT_scale=scales[:, a, g, :],
                     rhs=wih_codes[:, g, d, :].bitcast(FP8X4),
@@ -251,83 +259,120 @@ def tile_dependency_pa_t_kernel(
                     stop=(g == PASSES - 1),
                 )
             nc.vector.tensor_tensor(
-                out=gates_of[r][:, d, a, :], in0=mx_bank[:], in1=gates_of[r][:, d, a, :], op=ALU.add
+                out=gates_of[unit][:, a, :], in0=bank[:], in1=gates_of[unit][:, a, :], op=ALU.add
             )
 
-        def new_cell(r):
-            gates = gates_of[r]
+        def squash_gates(unit):
+            gates = gates_of[unit]
+            out_gate = triple.tile([P, ROUND, H], F32)
+            out_gate_of[unit] = out_gate
+            nc.scalar.activation(out=gates[:, :, 0 : 2 * H], in_=gates[:, :, 0 : 2 * H], func=ACT.Sigmoid)
+            nc.scalar.activation(out=gates[:, :, 2 * H : 3 * H], in_=gates[:, :, 2 * H : 3 * H], func=ACT.Tanh)
+            nc.scalar.activation(out=out_gate[:], in_=gates[:, :, 3 * H : 4 * H], func=ACT.Sigmoid)
+
+        def new_cell(unit):
+            gates = gates_of[unit]
+            r, d = units[unit]
             tiles = slice(r * ROUND, (r + 1) * ROUND)
-            nc.scalar.activation(out=gates[:, :, :, 0 : 2 * H], in_=gates[:, :, :, 0 : 2 * H], func=ACT.Sigmoid)
-            nc.scalar.activation(out=gates[:, :, :, 2 * H : 3 * H], in_=gates[:, :, :, 2 * H : 3 * H], func=ACT.Tanh)
-            out_gate = triple.tile([P, DIRS, ROUND, H], F32)
-            nc.scalar.activation(out=out_gate[:], in_=gates[:, :, :, 3 * H : 4 * H], func=ACT.Sigmoid)
-            out_gate_of[r] = out_gate
-            engine = nc.vector if r >= ROUNDS - VECTOR_ROUNDS else nc.gpsimd
-            kept = double.tile([P, DIRS, ROUND, H], F32)
+            engine = nc.vector if unit >= UNITS - VECTOR_UNITS else nc.gpsimd
+            kept = double.tile([P, ROUND, H], F32)
             engine.tensor_tensor(
-                out=kept[:], in0=gates[:, :, :, H : 2 * H], in1=c0_rows[:, :, tiles, :], op=ALU.mult
+                out=kept[:], in0=gates[:, :, H : 2 * H], in1=c0_rows[:, d, tiles, :], op=ALU.mult
             )
-            written = double.tile([P, DIRS, ROUND, H], F32)
+            written = double.tile([P, ROUND, H], F32)
             engine.tensor_tensor(
-                out=written[:], in0=gates[:, :, :, 0:H], in1=gates[:, :, :, 2 * H : 3 * H], op=ALU.mult
+                out=written[:], in0=gates[:, :, 0:H], in1=gates[:, :, 2 * H : 3 * H], op=ALU.mult
             )
-            cell = triple.tile([P, DIRS, ROUND, H], F32)
+            cell = triple.tile([P, ROUND, H], F32)
             engine.tensor_tensor(out=cell[:], in0=kept[:], in1=written[:], op=ALU.add)
-            cell_of[r] = cell
+            cell_of[unit] = cell
 
-        def squash_cell(r):
-            cell_tanh = double.tile([P, DIRS, ROUND, H], F32)
-            nc.scalar.activation(out=cell_tanh[:], in_=cell_of[r][:], func=ACT.Tanh)
-            cell_tanh_of[r] = cell_tanh
+        def squash_cell(unit):
+            cell_tanh = double.tile([P, ROUND, H], F32)
+            nc.scalar.activation(out=cell_tanh[:], in_=cell_of[unit][:], func=ACT.Tanh)
+            cell_tanh_of[unit] = cell_tanh
 
-        def new_hidden(r):
+        def new_hidden(unit):
+            r, d = units[unit]
             tiles = slice(r * ROUND, (r + 1) * ROUND)
-            hidden = triple.tile([P, ROUND, DIRS, H], F32)
-            nc.vector.tensor_tensor(
-                out=hidden[:].rearrange("p a d h -> p d a h"),
-                in0=out_gate_of[r][:],
-                in1=cell_tanh_of[r][:],
-                op=ALU.mult,
-            )
+            hidden = triple.tile([P, ROUND, H], F32)
+            nc.vector.tensor_tensor(out=hidden[:], in0=out_gate_of[unit][:], in1=cell_tanh_of[unit][:], op=ALU.mult)
             nc.sync.dma_start(
-                out=out.rearrange("(p t) (d h) -> p t d h", t=TILES, d=DIRS)[:, tiles, :, :],
+                out=out.rearrange("(p t) (d h) -> p t d h", t=TILES, d=DIRS)[:, tiles, d, :],
                 in_=hidden[:],
             )
 
-        for d in range(DIRS):
-            prepare_small_weights(d)
+        next_term = [0]
+
+        def recurrent_terms(count, on_scalar=False):
+            for _ in range(count):
+                recurrent_term(next_term[0], on_scalar)
+                next_term[0] += 1
+
+        for _ in range(WARM_MATMULS):
+            bank = banks.tile([P, GATES], F32)
+            nc.tensor.matmul(out=bank[:], lhsT=ones[:, 0:P], rhs=ones[:], start=True, stop=True)
+        prepare_small_weights(0)
         for r in range(2):
             flip_state(r)
             collect_state(r)
-        for d, a in blocks:
-            recurrent_term(0, d, a)
-        prepare_weights(0)
-        for r in range(2):
-            flip_features(r)
-            collect_features(r)
-            quantise_features(r)
-        prepare_weights(1)
+        recurrent_terms(4)
+        for q in range(4):
+            flip_weights(0, q)
+        prepare_small_weights(1)
+        quantise_weights(0)
+        for a in range(ROUND):
+            flip_features(0, a)
+            collect_features(0, a)
+        recurrent_terms(2)
+        quantise_features(0)
+        flip_state(2)
+        collect_state(2)
+        recurrent_terms(2)
+        for a in range(ROUND):
+            flip_features(1, a)
+            collect_features(1, a)
+        quantise_features(1)
+        for unit in range(2):
+            for a in range(ROUND):
+                input_term(unit, a)
+            for q in range(2 * unit, 2 * unit + 2):
+                flip_weights(1, q)
+            squash_gates(unit)
+            new_cell(unit)
+        quantise_weights(1)
 
-        for i in range(ROUNDS + 2):
-            load = i // LOAD_ROUNDS + LOADS_AHEAD
-            if i % LOAD_ROUNDS == 0 and load < LOADS:
-                load_tokens(load)
-            if 1 <= i <= ROUNDS:
-                new_cell(i - 1)
-            if i >= 2:
-                squash_cell(i - 2)
-            for d in range(DIRS):
-                for a in range(ROUND):
-                    if i < ROUNDS:
-                        input_term(i, d, a)
-                    if i + 1 < ROUNDS:
-                        recurrent_term(i + 1, d, a)
-                if d == 0 and i + 2 < ROUNDS:
-                    flip_features(i + 2)
-                    flip_state(i + 2)
-                    collect_features(i + 2)
-                    collect_state(i + 2)
-            if i >= 2:
-                new_hidden(i - 2)
-            if i + 2 < ROUNDS:
+        for u in range(UNITS + 1):
+            i, odd = divmod(u, 2)
+            if not odd and i + LOADS_AHEAD < ROUNDS:
+                load_features(i + LOADS_AHEAD)
+                if i == 2:
+                    load_state(h0_rows, h0, 20, TILES)
+                if i == 4:
+                    load_state(c0_rows, c0, 20, TILES)
+            if u > 2:
+                squash_gates(u - 1)
+            if LAG <= u < UNITS - HOLD:
+                squash_cell(u - LAG)
+            if odd and i + 2 < ROUNDS:
                 quantise_features(i + 2)
+            for a in range(ROUND):
+                if 2 <= u < UNITS:
+                    input_term(u, a)
+                recurrent_terms(1, on_scalar=(odd and a == 1))
+            if u > 2:
+                new_cell(u - 1)
+            if not odd and i + 2 < ROUNDS:
+                for a in range(ROUND):
+                    flip_features(i + 2, a)
+                if i + 3 < ROUNDS:
+                    flip_state(i + 3)
+                for a in range(ROUND):
+                    collect_features(i + 2, a)
+                if i + 3 < ROUNDS:
+                    collect_state(i + 3)
+            if LAG <= u < UNITS - HOLD:
+                new_hidden(u - LAG)
+        for unit in range(UNITS - HOLD - LAG, UNITS):
+            squash_cell(unit)
+            new_hidden(unit)

@@ -24,14 +24,13 @@ PASSES = IN0 // (P * PACK)
 TILES = S // P
 ROUND = 2
 ROUNDS = TILES // ROUND
-UNITS = ROUNDS * DIRS
-STREAM_LOADS = 8
+BOTH = slice(0, DIRS)
+ONE = [slice(d, d + 1) for d in range(DIRS)]
+HEAD_ROUNDS = 2
+STREAM_LOADS = 6
 LOADS_AHEAD = 5
 LAG = 3
-HOLD = 2
-LEAD = 2
 WARM_MATMULS = 6
-VECTOR_UNITS = 2
 
 FLOPS = 2 * S * (IN0 + H) * DIRS * GATES
 
@@ -59,11 +58,11 @@ def tile_dependency_pa_t_kernel(
     with ExitStack() as ctx:
         ctx.enter_context(tc.manual_schedule())
         keep = ctx.enter_context(tc.tile_pool(name="keep", bufs=1))
-        double = ctx.enter_context(tc.tile_pool(name="double", bufs=4))
-        triple = ctx.enter_context(tc.tile_pool(name="triple", bufs=8))
+        double = ctx.enter_context(tc.tile_pool(name="double", bufs=2))
+        stage = ctx.enter_context(tc.tile_pool(name="stage", bufs=4))
         stream = ctx.enter_context(tc.tile_pool(name="stream", bufs=STREAM_LOADS))
-        state_pool = ctx.enter_context(tc.tile_pool(name="state_pool", bufs=LEAD + 3))
-        gate_pool = ctx.enter_context(tc.tile_pool(name="gate_pool", bufs=2 * LEAD + 5))
+        state_pool = ctx.enter_context(tc.tile_pool(name="state_pool", bufs=6))
+        gate_pool = ctx.enter_context(tc.tile_pool(name="gate_pool", bufs=7))
         banks = ctx.enter_context(tc.psum_pool(name="banks", bufs=8))
 
         identity_bf16 = keep.tile([P, P], BF16)
@@ -122,15 +121,15 @@ def tile_dependency_pa_t_kernel(
 
         load_small_weights(0)
         load_state(h0_rows, h0, 0, 4)
-        load_weights(0)
-        load_features(0)
         load_small_weights(1)
-        load_state(h0_rows, h0, 4, 8)
+        load_weights(0)
+        load_state(h0_rows, h0, 4, 12)
+        load_features(0)
         load_features(1)
         load_weights(1)
-        load_features(2)
         load_state(c0_rows, c0, 0, 8)
-        load_state(h0_rows, h0, 8, 20)
+        load_features(2)
+        load_state(h0_rows, h0, 12, 22)
         for r in range(3, LOADS_AHEAD):
             load_features(r)
         load_state(c0_rows, c0, 8, 20)
@@ -148,6 +147,12 @@ def tile_dependency_pa_t_kernel(
         out_gate_of = {}
         cell_of = {}
         cell_tanh_of = {}
+        hidden_of = {}
+        terms_done = []
+
+        def warm_up():
+            bank = banks.tile([P, GATES], F32)
+            nc.tensor.matmul(out=bank[:], lhsT=ones[:, 0:P], rhs=ones[:], start=True, stop=True)
 
         def prepare_small_weights(d):
             bank = banks.tile([P, 4, P], BF16)
@@ -205,8 +210,8 @@ def tile_dependency_pa_t_kernel(
             nc.scalar.copy(out=grouped_words[:, a], in_=flipped_of[r, a])
 
         def quantise_features(r):
-            codes = triple.tile([P, ROUND, PASSES, P], U32, align_bytes=64)
-            scales = triple.tile([P, ROUND, PASSES, P], U8, align_bytes=64)
+            codes = stage.tile([P, ROUND, PASSES, P], U32, align_bytes=64)
+            scales = stage.tile([P, ROUND, PASSES, P], U8, align_bytes=64)
             nc.vector.quantize_mx(
                 out=codes[:].rearrange("p a g r -> p (a g r)").bitcast(FP8X4),
                 scales=scales[:].rearrange("p a g r -> p (a g r)"),
@@ -214,18 +219,16 @@ def tile_dependency_pa_t_kernel(
             )
             operand_of[r] = (codes, scales)
 
-        units = [(r, d) for d in range(DIRS) for r in range(2)]
-        units += [(r, d) for r in range(2, ROUNDS) for d in range(DIRS)]
-        terms = [(unit, a) for unit in range(UNITS) for a in range(ROUND)]
+        blocks = [(d, a) for d in range(DIRS) for a in range(ROUND)]
+        terms = [(r, d, a) for d in range(DIRS) for r in range(HEAD_ROUNDS) for a in range(ROUND)]
+        terms += [(r, d, a) for r in range(HEAD_ROUNDS, ROUNDS) for d, a in blocks]
 
-        def recurrent_term(index, on_scalar):
-            if index >= len(terms):
-                return
-            unit, a = terms[index]
-            r, d = units[unit]
-            if a == 0:
-                gates = gate_pool.tile([P, ROUND, GATES], F32)
-                gates_of[unit] = gates
+        def recurrent_term(on_scalar=False):
+            r, d, a = terms[len(terms_done)]
+            terms_done.append((r, d, a))
+            if r not in gates_of:
+                gates = gate_pool.tile([P, DIRS, ROUND, GATES], F32)
+                gates_of[r] = gates
             bank = banks.tile([P, GATES], F32)
             nc.tensor.matmul(
                 out=bank[:],
@@ -238,14 +241,13 @@ def tile_dependency_pa_t_kernel(
                 nc.tensor.matmul(
                     out=bank[:], lhsT=ones[:, 0:P], rhs=bias_rows[:, d, :], start=False, stop=True
                 )
-                nc.scalar.copy(out=gates_of[unit][:, a, :], in_=bank[:])
+                nc.scalar.copy(out=gates_of[r][:, d, a, :], in_=bank[:])
             else:
                 nc.vector.tensor_tensor(
-                    out=gates_of[unit][:, a, :], in0=bank[:], in1=bias[:, d, :], op=ALU.add
+                    out=gates_of[r][:, d, a, :], in0=bank[:], in1=bias[:, d, :], op=ALU.add
                 )
 
-        def input_term(unit, a):
-            r, d = units[unit]
+        def input_term(r, d, a):
             codes, scales = operand_of[r]
             bank = banks.tile([P, GATES], F32)
             for g in range(PASSES):
@@ -259,120 +261,151 @@ def tile_dependency_pa_t_kernel(
                     stop=(g == PASSES - 1),
                 )
             nc.vector.tensor_tensor(
-                out=gates_of[unit][:, a, :], in0=bank[:], in1=gates_of[unit][:, a, :], op=ALU.add
+                out=gates_of[r][:, d, a, :], in0=bank[:], in1=gates_of[r][:, d, a, :], op=ALU.add
             )
 
-        def squash_gates(unit):
-            gates = gates_of[unit]
-            out_gate = triple.tile([P, ROUND, H], F32)
-            out_gate_of[unit] = out_gate
-            nc.scalar.activation(out=gates[:, :, 0 : 2 * H], in_=gates[:, :, 0 : 2 * H], func=ACT.Sigmoid)
-            nc.scalar.activation(out=gates[:, :, 2 * H : 3 * H], in_=gates[:, :, 2 * H : 3 * H], func=ACT.Tanh)
-            nc.scalar.activation(out=out_gate[:], in_=gates[:, :, 3 * H : 4 * H], func=ACT.Sigmoid)
+        def squash_gates(r, dirs):
+            gates = gates_of[r][:, dirs]
+            if r not in out_gate_of:
+                out_gate = stage.tile([P, DIRS, ROUND, H], F32)
+                out_gate_of[r] = out_gate
+            nc.scalar.activation(out=gates[:, :, :, 0 : 2 * H], in_=gates[:, :, :, 0 : 2 * H], func=ACT.Sigmoid)
+            nc.scalar.activation(out=gates[:, :, :, 2 * H : 3 * H], in_=gates[:, :, :, 2 * H : 3 * H], func=ACT.Tanh)
+            nc.scalar.activation(out=out_gate_of[r][:, dirs], in_=gates[:, :, :, 3 * H : 4 * H], func=ACT.Sigmoid)
 
-        def new_cell(unit):
-            gates = gates_of[unit]
-            r, d = units[unit]
+        def cell_products(r, dirs, engine):
+            gates = gates_of[r][:, dirs]
             tiles = slice(r * ROUND, (r + 1) * ROUND)
-            engine = nc.vector if unit >= UNITS - VECTOR_UNITS else nc.gpsimd
-            kept = double.tile([P, ROUND, H], F32)
+            if r not in cell_of:
+                kept = double.tile([P, DIRS, ROUND, H], F32)
+                written = double.tile([P, DIRS, ROUND, H], F32)
+                cell = stage.tile([P, DIRS, ROUND, H], F32)
+                cell_of[r] = (kept, written, cell)
+            kept, written, cell = cell_of[r]
             engine.tensor_tensor(
-                out=kept[:], in0=gates[:, :, H : 2 * H], in1=c0_rows[:, d, tiles, :], op=ALU.mult
+                out=kept[:, dirs], in0=gates[:, :, :, H : 2 * H], in1=c0_rows[:, dirs, tiles, :], op=ALU.mult
             )
-            written = double.tile([P, ROUND, H], F32)
             engine.tensor_tensor(
-                out=written[:], in0=gates[:, :, 0:H], in1=gates[:, :, 2 * H : 3 * H], op=ALU.mult
+                out=written[:, dirs], in0=gates[:, :, :, 0:H], in1=gates[:, :, :, 2 * H : 3 * H], op=ALU.mult
             )
-            cell = triple.tile([P, ROUND, H], F32)
-            engine.tensor_tensor(out=cell[:], in0=kept[:], in1=written[:], op=ALU.add)
-            cell_of[unit] = cell
 
-        def squash_cell(unit):
-            cell_tanh = double.tile([P, ROUND, H], F32)
-            nc.scalar.activation(out=cell_tanh[:], in_=cell_of[unit][:], func=ACT.Tanh)
-            cell_tanh_of[unit] = cell_tanh
+        def cell_sum(r, dirs, engine):
+            kept, written, cell = cell_of[r]
+            engine.tensor_tensor(out=cell[:, dirs], in0=kept[:, dirs], in1=written[:, dirs], op=ALU.add)
 
-        def new_hidden(unit):
-            r, d = units[unit]
+        def squash_cell(r, dirs):
+            if r not in cell_tanh_of:
+                cell_tanh = double.tile([P, DIRS, ROUND, H], F32)
+                cell_tanh_of[r] = cell_tanh
+            nc.scalar.activation(out=cell_tanh_of[r][:, dirs], in_=cell_of[r][2][:, dirs], func=ACT.Tanh)
+
+        def new_hidden(r, dirs):
             tiles = slice(r * ROUND, (r + 1) * ROUND)
-            hidden = triple.tile([P, ROUND, H], F32)
-            nc.vector.tensor_tensor(out=hidden[:], in0=out_gate_of[unit][:], in1=cell_tanh_of[unit][:], op=ALU.mult)
+            if r not in hidden_of:
+                hidden = stage.tile([P, ROUND, DIRS, H], F32)
+                hidden_of[r] = hidden
+            rows = hidden_of[r][:, :, dirs]
+            nc.vector.tensor_tensor(
+                out=rows.rearrange("p a d h -> p d a h"),
+                in0=out_gate_of[r][:, dirs],
+                in1=cell_tanh_of[r][:, dirs],
+                op=ALU.mult,
+            )
             nc.sync.dma_start(
-                out=out.rearrange("(p t) (d h) -> p t d h", t=TILES, d=DIRS)[:, tiles, d, :],
-                in_=hidden[:],
+                out=out.rearrange("(p t) (d h) -> p t d h", t=TILES, d=DIRS)[:, tiles, dirs, :], in_=rows
             )
-
-        next_term = [0]
-
-        def recurrent_terms(count, on_scalar=False):
-            for _ in range(count):
-                recurrent_term(next_term[0], on_scalar)
-                next_term[0] += 1
 
         for _ in range(WARM_MATMULS):
-            bank = banks.tile([P, GATES], F32)
-            nc.tensor.matmul(out=bank[:], lhsT=ones[:, 0:P], rhs=ones[:], start=True, stop=True)
+            warm_up()
         prepare_small_weights(0)
-        for r in range(2):
+        warm_up()
+        for r in range(HEAD_ROUNDS):
             flip_state(r)
             collect_state(r)
-        recurrent_terms(4)
+        prepare_small_weights(1)
+        for _ in blocks:
+            recurrent_term()
         for q in range(4):
             flip_weights(0, q)
-        prepare_small_weights(1)
+            recurrent_term()
         quantise_weights(0)
-        for a in range(ROUND):
-            flip_features(0, a)
-            collect_features(0, a)
-        recurrent_terms(2)
-        quantise_features(0)
-        flip_state(2)
-        collect_state(2)
-        recurrent_terms(2)
-        for a in range(ROUND):
-            flip_features(1, a)
-            collect_features(1, a)
-        quantise_features(1)
-        for unit in range(2):
+        for r in range(HEAD_ROUNDS, 2 * HEAD_ROUNDS):
+            flip_state(r)
+            collect_state(r)
+        for r in range(HEAD_ROUNDS):
             for a in range(ROUND):
-                input_term(unit, a)
-            for q in range(2 * unit, 2 * unit + 2):
-                flip_weights(1, q)
-            squash_gates(unit)
-            new_cell(unit)
+                flip_features(r, a)
+                collect_features(r, a)
+                recurrent_term()
+            quantise_features(r)
+        for r in range(HEAD_ROUNDS):
+            for a in range(ROUND):
+                input_term(r, 0, a)
+                flip_weights(1, 2 * r + a)
+                if r > 0:
+                    recurrent_term()
+            squash_gates(r, ONE[0])
+            cell_products(r, ONE[0], nc.gpsimd)
+            cell_sum(r, ONE[0], nc.gpsimd)
+        flip_state(4)
+        collect_state(4)
         quantise_weights(1)
 
-        for u in range(UNITS + 1):
-            i, odd = divmod(u, 2)
-            if not odd and i + LOADS_AHEAD < ROUNDS:
+        states = 5
+        last = ROUNDS - 1
+        head_terms = len(terms_done)
+        for i in range(last):
+            due = min(len(terms), head_terms + (len(terms) - head_terms) * (i + 1) / (ROUNDS - 2))
+            if i + LOADS_AHEAD < ROUNDS:
                 load_features(i + LOADS_AHEAD)
                 if i == 2:
-                    load_state(h0_rows, h0, 20, TILES)
+                    load_state(h0_rows, h0, 22, TILES)
                 if i == 4:
                     load_state(c0_rows, c0, 20, TILES)
-            if u > 2:
-                squash_gates(u - 1)
-            if LAG <= u < UNITS - HOLD:
-                squash_cell(u - LAG)
-            if odd and i + 2 < ROUNDS:
+            if i >= 1:
+                dirs = ONE[1] if i - 1 < HEAD_ROUNDS else BOTH
+                squash_gates(i - 1, dirs)
+                cell_products(i - 1, dirs, nc.gpsimd)
+                cell_sum(i - 1, dirs, nc.gpsimd)
+            if i >= 2:
+                squash_cell(i - 2, BOTH)
+            if i >= LAG:
+                new_hidden(i - LAG, BOTH)
+            for k, (d, a) in enumerate(blocks):
+                if d == 1 or i >= HEAD_ROUNDS:
+                    input_term(i, d, a)
+                if len(terms_done) < due:
+                    recurrent_term(on_scalar=(k == 2))
+                if k == 1:
+                    if states <= terms[min(len(terms_done) + 5, len(terms) - 1)][0]:
+                        flip_state(states)
+                        collect_state(states)
+                        states += 1
+                    if i + 2 < ROUNDS:
+                        for b in range(ROUND):
+                            flip_features(i + 2, b)
+                        for b in range(ROUND):
+                            collect_features(i + 2, b)
+            if i + 2 < ROUNDS:
                 quantise_features(i + 2)
+
+        squash_gates(last - 1, BOTH)
+        for d in range(DIRS):
             for a in range(ROUND):
-                if 2 <= u < UNITS:
-                    input_term(u, a)
-                recurrent_terms(1, on_scalar=(odd and a == 1))
-            if u > 2:
-                new_cell(u - 1)
-            if not odd and i + 2 < ROUNDS:
-                for a in range(ROUND):
-                    flip_features(i + 2, a)
-                if i + 3 < ROUNDS:
-                    flip_state(i + 3)
-                for a in range(ROUND):
-                    collect_features(i + 2, a)
-                if i + 3 < ROUNDS:
-                    collect_state(i + 3)
-            if LAG <= u < UNITS - HOLD:
-                new_hidden(u - LAG)
-        for unit in range(UNITS - HOLD - LAG, UNITS):
-            squash_cell(unit)
-            new_hidden(unit)
+                input_term(last, d, a)
+            squash_gates(last, ONE[d])
+            if d == 0:
+                squash_cell(last - 2, BOTH)
+        new_hidden(last - 3, BOTH)
+        cell_products(last - 1, BOTH, nc.vector)
+        new_hidden(last - 2, BOTH)
+        cell_sum(last - 1, BOTH, nc.vector)
+        squash_cell(last - 1, BOTH)
+        for d in range(DIRS):
+            cell_products(last, ONE[d], nc.vector)
+        for d in range(DIRS):
+            cell_sum(last, ONE[d], nc.vector)
+            squash_cell(last, ONE[d])
+        new_hidden(last - 1, BOTH)
+        for d in range(DIRS):
+            new_hidden(last, ONE[d])

@@ -24,12 +24,13 @@ PASSES = IN0 // (P * PACK)
 TILES = S // P
 ROUND = 2
 ROUNDS = TILES // ROUND
-BOTH = slice(0, DIRS)
-ONE = [slice(d, d + 1) for d in range(DIRS)]
+BLOCKS = DIRS * ROUND
+TURNED = BLOCKS - 1
 HEAD_ROUNDS = 2
 STREAM_LOADS = 6
 LOADS_AHEAD = 5
 LAG = 3
+HEAD_STATES = 5
 WARM_MATMULS = 6
 
 FLOPS = 2 * S * (IN0 + H) * DIRS * GATES
@@ -61,7 +62,7 @@ def tile_dependency_pa_t_kernel(
         double = ctx.enter_context(tc.tile_pool(name="double", bufs=2))
         stage = ctx.enter_context(tc.tile_pool(name="stage", bufs=4))
         stream = ctx.enter_context(tc.tile_pool(name="stream", bufs=STREAM_LOADS))
-        state_pool = ctx.enter_context(tc.tile_pool(name="state_pool", bufs=6))
+        state_pool = ctx.enter_context(tc.tile_pool(name="state_pool", bufs=8))
         gate_pool = ctx.enter_context(tc.tile_pool(name="gate_pool", bufs=7))
         banks = ctx.enter_context(tc.psum_pool(name="banks", bufs=8))
 
@@ -136,6 +137,7 @@ def tile_dependency_pa_t_kernel(
 
         whh_t = keep.tile([P, DIRS, 4, H], BF16)
         bias = keep.tile([P, DIRS, GATES], F32)
+        bias_column = keep.tile([P, 4], F32)
         wih_codes = keep.tile([P, PASSES, DIRS, GATES], U32, align_bytes=64)
         wih_scales = keep.tile([P, PASSES, DIRS, GATES], U8, align_bytes=64)
         state_bank_of = {}
@@ -149,6 +151,8 @@ def tile_dependency_pa_t_kernel(
         cell_tanh_of = {}
         hidden_of = {}
         terms_done = []
+        turned_of = {}
+        turned_bank_of = {}
 
         def warm_up():
             bank = banks.tile([P, GATES], F32)
@@ -162,6 +166,12 @@ def tile_dependency_pa_t_kernel(
             bank = banks.tile([P, GATES], F32)
             nc.tensor.matmul(out=bank[:], lhsT=ones[:, 0:P], rhs=bias_rows[:, d, :], start=True, stop=True)
             nc.scalar.copy(out=bias[:, d, :], in_=bank[:])
+
+        def prepare_bias_column():
+            bank = banks.tile([P, 4, P], F32)
+            for q in range(4):
+                nc.tensor.transpose(bank[:, q, :], bias[:, 1, q * P : (q + 1) * P], identity_f32[:])
+            nc.scalar.copy(out=bias_column[:], in_=bank[:, :, 0])
 
         wih_grouped_of = {}
 
@@ -220,34 +230,34 @@ def tile_dependency_pa_t_kernel(
             operand_of[r] = (codes, scales)
 
         blocks = [(d, a) for d in range(DIRS) for a in range(ROUND)]
-        terms = [(r, d, a) for d in range(DIRS) for r in range(HEAD_ROUNDS) for a in range(ROUND)]
-        terms += [(r, d, a) for r in range(HEAD_ROUNDS, ROUNDS) for d, a in blocks]
+        terms = [(r, b) for d in range(DIRS) for r in range(HEAD_ROUNDS) for b in (2 * d, 2 * d + 1)]
+        terms += [(r, b) for r in range(HEAD_ROUNDS, ROUNDS) for b in range(TURNED)]
 
-        def recurrent_term(on_scalar=False):
-            r, d, a = terms[len(terms_done)]
-            terms_done.append((r, d, a))
-            if r not in gates_of:
-                gates = gate_pool.tile([P, DIRS, ROUND, GATES], F32)
-                gates_of[r] = gates
+        def recurrent_product(r, b, stop):
+            d, a = blocks[b]
             bank = banks.tile([P, GATES], F32)
             nc.tensor.matmul(
                 out=bank[:],
                 lhsT=h0_t_of[r][:, d, a, :],
                 rhs=whh_t[:, d].rearrange("p r h -> p (r h)"),
                 start=True,
-                stop=not on_scalar,
+                stop=stop,
             )
-            if on_scalar:
-                nc.tensor.matmul(
-                    out=bank[:], lhsT=ones[:, 0:P], rhs=bias_rows[:, d, :], start=False, stop=True
-                )
-                nc.scalar.copy(out=gates_of[r][:, d, a, :], in_=bank[:])
-            else:
-                nc.vector.tensor_tensor(
-                    out=gates_of[r][:, d, a, :], in0=bank[:], in1=bias[:, d, :], op=ALU.add
-                )
+            return bank
 
-        def input_term(r, d, a):
+        def recurrent_term():
+            r, b = terms[len(terms_done)]
+            terms_done.append((r, b))
+            if r not in gates_of:
+                gates = gate_pool.tile([P, BLOCKS, GATES], F32)
+                gates_of[r] = gates
+            bank = recurrent_product(r, b, True)
+            nc.vector.tensor_tensor(
+                out=gates_of[r][:, b, :], in0=bank[:], in1=bias[:, b // ROUND, :], op=ALU.add
+            )
+
+        def input_term(r, b):
+            d, a = blocks[b]
             codes, scales = operand_of[r]
             bank = banks.tile([P, GATES], F32)
             for g in range(PASSES):
@@ -261,54 +271,106 @@ def tile_dependency_pa_t_kernel(
                     stop=(g == PASSES - 1),
                 )
             nc.vector.tensor_tensor(
-                out=gates_of[r][:, d, a, :], in0=bank[:], in1=gates_of[r][:, d, a, :], op=ALU.add
+                out=gates_of[r][:, b, :], in0=bank[:], in1=gates_of[r][:, b, :], op=ALU.add
             )
 
-        def squash_gates(r, dirs):
-            gates = gates_of[r][:, dirs]
-            if r not in out_gate_of:
-                out_gate = stage.tile([P, DIRS, ROUND, H], F32)
-                out_gate_of[r] = out_gate
-            nc.scalar.activation(out=gates[:, :, :, 0 : 2 * H], in_=gates[:, :, :, 0 : 2 * H], func=ACT.Sigmoid)
-            nc.scalar.activation(out=gates[:, :, :, 2 * H : 3 * H], in_=gates[:, :, :, 2 * H : 3 * H], func=ACT.Tanh)
-            nc.scalar.activation(out=out_gate_of[r][:, dirs], in_=gates[:, :, :, 3 * H : 4 * H], func=ACT.Sigmoid)
+        def turned_products(r):
+            a = TURNED % ROUND
+            codes, scales = operand_of[r]
+            bank = banks.tile([P, 4, P], F32)
+            for q in range(4):
+                columns = slice(q * P, (q + 1) * P)
+                for g in range(PASSES):
+                    nc.tensor.matmul_mx(
+                        out=bank[:, q, :],
+                        lhsT=wih_codes[:, g, TURNED // ROUND, columns].bitcast(FP8X4),
+                        lhsT_scale=wih_scales[:, g, TURNED // ROUND, columns],
+                        rhs=codes[:, a, g, :].bitcast(FP8X4),
+                        rhs_scale=scales[:, a, g, :],
+                        start=(g == 0),
+                        stop=(g == PASSES - 1),
+                    )
+            turned = double.tile([P, 4, P], F32)
+            for q in range(4):
+                nc.scalar.activation(
+                    out=turned[:, q, :], in_=bank[:, q, :], func=ACT.Identity, bias=bias_column[:, q : q + 1]
+                )
+            turned_of[r] = turned
 
-        def cell_products(r, dirs, engine):
-            gates = gates_of[r][:, dirs]
+        def turned_sum(r):
+            bank = recurrent_product(r, TURNED, False)
+            for q in range(4):
+                nc.tensor.matmul(
+                    out=bank[:, q * P : (q + 1) * P],
+                    lhsT=turned_of[r][:, q, :],
+                    rhs=identity_f32[:],
+                    start=False,
+                    stop=(q == 3),
+                    is_transpose=True,
+                )
+            turned_bank_of[r] = bank
+
+        def squash(r, part, source):
+            gates = gates_of[r][:, part]
+            if r not in out_gate_of:
+                out_gate = stage.tile([P, BLOCKS, H], F32)
+                out_gate_of[r] = out_gate
+            nc.scalar.activation(out=gates[:, :, 0 : 2 * H], in_=source[:, :, 0 : 2 * H], func=ACT.Sigmoid)
+            nc.scalar.activation(out=gates[:, :, 2 * H : 3 * H], in_=source[:, :, 2 * H : 3 * H], func=ACT.Tanh)
+            nc.scalar.activation(out=out_gate_of[r][:, part], in_=source[:, :, 3 * H : 4 * H], func=ACT.Sigmoid)
+
+        def squash_gates(r, first, last):
+            squash(r, slice(first, last), gates_of[r][:, first:last])
+
+        def squash_turned(r):
+            squash(r, slice(TURNED, TURNED + 1), turned_bank_of[r][:].rearrange("p (b n) -> p b n", b=1))
+
+        def cell_products(r, first, last, engine):
+            part = slice(first, last)
+            gates = gates_of[r][:, part]
             tiles = slice(r * ROUND, (r + 1) * ROUND)
+            dirs = slice(first // ROUND, (last + ROUND - 1) // ROUND)
             if r not in cell_of:
-                kept = double.tile([P, DIRS, ROUND, H], F32)
-                written = double.tile([P, DIRS, ROUND, H], F32)
-                cell = stage.tile([P, DIRS, ROUND, H], F32)
+                kept = double.tile([P, BLOCKS, H], F32)
+                written = double.tile([P, BLOCKS, H], F32)
+                cell = stage.tile([P, BLOCKS, H], F32)
                 cell_of[r] = (kept, written, cell)
             kept, written, cell = cell_of[r]
             engine.tensor_tensor(
-                out=kept[:, dirs], in0=gates[:, :, :, H : 2 * H], in1=c0_rows[:, dirs, tiles, :], op=ALU.mult
+                out=kept[:, part].rearrange("p (d a) h -> p d a h", a=ROUND),
+                in0=gates[:, :, H : 2 * H].rearrange("p (d a) h -> p d a h", a=ROUND),
+                in1=c0_rows[:, dirs, tiles, :],
+                op=ALU.mult,
             )
             engine.tensor_tensor(
-                out=written[:, dirs], in0=gates[:, :, :, 0:H], in1=gates[:, :, :, 2 * H : 3 * H], op=ALU.mult
+                out=written[:, part], in0=gates[:, :, 0:H], in1=gates[:, :, 2 * H : 3 * H], op=ALU.mult
             )
 
-        def cell_sum(r, dirs, engine):
+        def cell_sum(r, first, last, engine):
             kept, written, cell = cell_of[r]
-            engine.tensor_tensor(out=cell[:, dirs], in0=kept[:, dirs], in1=written[:, dirs], op=ALU.add)
+            engine.tensor_tensor(out=cell[:, first:last], in0=kept[:, first:last], in1=written[:, first:last], op=ALU.add)
 
-        def squash_cell(r, dirs):
+        def new_cell(r, first, last, engine):
+            cell_products(r, first, last, engine)
+            cell_sum(r, first, last, engine)
+
+        def squash_cell(r, first, last):
             if r not in cell_tanh_of:
-                cell_tanh = double.tile([P, DIRS, ROUND, H], F32)
+                cell_tanh = double.tile([P, BLOCKS, H], F32)
                 cell_tanh_of[r] = cell_tanh
-            nc.scalar.activation(out=cell_tanh_of[r][:, dirs], in_=cell_of[r][2][:, dirs], func=ACT.Tanh)
+            nc.scalar.activation(out=cell_tanh_of[r][:, first:last], in_=cell_of[r][2][:, first:last], func=ACT.Tanh)
 
-        def new_hidden(r, dirs):
+        def new_hidden(r, first, last):
             tiles = slice(r * ROUND, (r + 1) * ROUND)
+            dirs = slice(first // ROUND, (last + ROUND - 1) // ROUND)
             if r not in hidden_of:
                 hidden = stage.tile([P, ROUND, DIRS, H], F32)
                 hidden_of[r] = hidden
             rows = hidden_of[r][:, :, dirs]
             nc.vector.tensor_tensor(
                 out=rows.rearrange("p a d h -> p d a h"),
-                in0=out_gate_of[r][:, dirs],
-                in1=cell_tanh_of[r][:, dirs],
+                in0=out_gate_of[r][:, first:last].rearrange("p (d a) h -> p d a h", a=ROUND),
+                in1=cell_tanh_of[r][:, first:last].rearrange("p (d a) h -> p d a h", a=ROUND),
                 op=ALU.mult,
             )
             nc.sync.dma_start(
@@ -325,11 +387,12 @@ def tile_dependency_pa_t_kernel(
         prepare_small_weights(1)
         for _ in blocks:
             recurrent_term()
+        prepare_bias_column()
         for q in range(4):
             flip_weights(0, q)
             recurrent_term()
         quantise_weights(0)
-        for r in range(HEAD_ROUNDS, 2 * HEAD_ROUNDS):
+        for r in range(HEAD_ROUNDS, HEAD_STATES):
             flip_state(r)
             collect_state(r)
         for r in range(HEAD_ROUNDS):
@@ -340,18 +403,20 @@ def tile_dependency_pa_t_kernel(
             quantise_features(r)
         for r in range(HEAD_ROUNDS):
             for a in range(ROUND):
-                input_term(r, 0, a)
+                input_term(r, a)
                 flip_weights(1, 2 * r + a)
                 if r > 0:
                     recurrent_term()
-            squash_gates(r, ONE[0])
-            cell_products(r, ONE[0], nc.gpsimd)
-            cell_sum(r, ONE[0], nc.gpsimd)
-        flip_state(4)
-        collect_state(4)
+            squash_gates(r, 0, ROUND)
+            cell_products(r, 0, ROUND, nc.gpsimd)
+            cell_sum(r, 0, ROUND, nc.gpsimd)
         quantise_weights(1)
 
-        states = 5
+        def recurrent_terms(due):
+            if len(terms_done) < due:
+                recurrent_term()
+
+        states = HEAD_STATES
         last = ROUNDS - 1
         head_terms = len(terms_done)
         for i in range(last):
@@ -362,50 +427,64 @@ def tile_dependency_pa_t_kernel(
                     load_state(h0_rows, h0, 22, TILES)
                 if i == 4:
                     load_state(c0_rows, c0, 20, TILES)
-            if i >= 1:
-                dirs = ONE[1] if i - 1 < HEAD_ROUNDS else BOTH
-                squash_gates(i - 1, dirs)
-                cell_products(i - 1, dirs, nc.gpsimd)
-                cell_sum(i - 1, dirs, nc.gpsimd)
+            early, late = ((2,), (3,)) if i < HEAD_ROUNDS else ((0, 1), (2,))
+            if 1 <= i <= HEAD_ROUNDS:
+                squash_gates(i - 1, ROUND, BLOCKS)
+                new_cell(i - 1, ROUND, BLOCKS, nc.gpsimd)
+            elif i > HEAD_ROUNDS:
+                turned_sum(i - 1)
+                squash_turned(i - 1)
+                squash_gates(i - 1, 0, TURNED)
+                new_cell(i - 1, 0, BLOCKS, nc.gpsimd)
             if i >= 2:
-                squash_cell(i - 2, BOTH)
+                squash_cell(i - 2, 0, BLOCKS)
             if i >= LAG:
-                new_hidden(i - LAG, BOTH)
-            for k, (d, a) in enumerate(blocks):
-                if d == 1 or i >= HEAD_ROUNDS:
-                    input_term(i, d, a)
-                if len(terms_done) < due:
-                    recurrent_term(on_scalar=(k == 2))
-                if k == 1:
-                    if states <= terms[min(len(terms_done) + 5, len(terms) - 1)][0]:
-                        flip_state(states)
-                        collect_state(states)
-                        states += 1
-                    if i + 2 < ROUNDS:
-                        for b in range(ROUND):
-                            flip_features(i + 2, b)
-                        for b in range(ROUND):
-                            collect_features(i + 2, b)
+                new_hidden(i - LAG, 0, BLOCKS)
+            for b in early:
+                input_term(i, b)
+            recurrent_terms(due)
+            needed = max(terms[min(len(terms_done) + 5, len(terms) - 1)][0], min(i + 2, last))
+            if states <= needed:
+                flip_state(states)
+                collect_state(states)
+                states += 1
+            if i + 2 < ROUNDS:
+                for a in range(ROUND):
+                    flip_features(i + 2, a)
+                collect_features(i + 2, 0)
+            recurrent_terms(due)
+            if i + 2 < ROUNDS:
+                collect_features(i + 2, 1)
+            for b in late:
+                input_term(i, b)
+            recurrent_terms(due)
+            if i + 1 >= HEAD_ROUNDS:
+                turned_products(i + 1)
             if i + 2 < ROUNDS:
                 quantise_features(i + 2)
 
-        squash_gates(last - 1, BOTH)
+        turned_sum(last - 1)
+        squash_turned(last - 1)
+        squash_gates(last - 1, 0, TURNED)
+        turned_sum(last)
+        squash_turned(last)
+        for b in range(ROUND):
+            input_term(last, b)
+        squash_gates(last, 0, ROUND)
+        squash_cell(last - 2, 0, BLOCKS)
+        for b in range(ROUND, TURNED):
+            input_term(last, b)
+        squash_gates(last, ROUND, TURNED)
+        new_hidden(last - 3, 0, BLOCKS)
+        cell_products(last - 1, 0, BLOCKS, nc.vector)
+        new_hidden(last - 2, 0, BLOCKS)
+        cell_sum(last - 1, 0, BLOCKS, nc.vector)
+        squash_cell(last - 1, 0, BLOCKS)
         for d in range(DIRS):
-            for a in range(ROUND):
-                input_term(last, d, a)
-            squash_gates(last, ONE[d])
-            if d == 0:
-                squash_cell(last - 2, BOTH)
-        new_hidden(last - 3, BOTH)
-        cell_products(last - 1, BOTH, nc.vector)
-        new_hidden(last - 2, BOTH)
-        cell_sum(last - 1, BOTH, nc.vector)
-        squash_cell(last - 1, BOTH)
+            cell_products(last, d * ROUND, (d + 1) * ROUND, nc.vector)
         for d in range(DIRS):
-            cell_products(last, ONE[d], nc.vector)
+            cell_sum(last, d * ROUND, (d + 1) * ROUND, nc.vector)
+            squash_cell(last, d * ROUND, (d + 1) * ROUND)
+        new_hidden(last - 1, 0, BLOCKS)
         for d in range(DIRS):
-            cell_sum(last, ONE[d], nc.vector)
-            squash_cell(last, ONE[d])
-        new_hidden(last - 1, BOTH)
-        for d in range(DIRS):
-            new_hidden(last, ONE[d])
+            new_hidden(last, d * ROUND, (d + 1) * ROUND)

@@ -31,6 +31,7 @@ STREAM_LOADS = 6
 LOADS_AHEAD = 5
 LAG = 3
 HEAD_STATES = 5
+SPLIT_ROUNDS = 13
 WARM_MATMULS = 6
 
 FLOPS = 2 * S * (IN0 + H) * DIRS * GATES
@@ -350,10 +351,6 @@ def tile_dependency_pa_t_kernel(
             kept, written, cell = cell_of[r]
             engine.tensor_tensor(out=cell[:, first:last], in0=kept[:, first:last], in1=written[:, first:last], op=ALU.add)
 
-        def new_cell(r, first, last, engine):
-            cell_products(r, first, last, engine)
-            cell_sum(r, first, last, engine)
-
         def squash_cell(r, first, last):
             if r not in cell_tanh_of:
                 cell_tanh = double.tile([P, BLOCKS, H], F32)
@@ -385,32 +382,38 @@ def tile_dependency_pa_t_kernel(
             flip_state(r)
             collect_state(r)
         prepare_small_weights(1)
-        for _ in blocks:
+        for _ in range(BLOCKS):
             recurrent_term()
-        prepare_bias_column()
         for q in range(4):
             flip_weights(0, q)
             recurrent_term()
         quantise_weights(0)
-        for r in range(HEAD_ROUNDS, HEAD_STATES):
+        for r in range(HEAD_ROUNDS, 2 * HEAD_ROUNDS):
             flip_state(r)
             collect_state(r)
+        prepare_bias_column()
         for r in range(HEAD_ROUNDS):
             for a in range(ROUND):
                 flip_features(r, a)
                 collect_features(r, a)
                 recurrent_term()
+                if (r, a) == (0, 0):
+                    warm_up()
             quantise_features(r)
         for r in range(HEAD_ROUNDS):
             for a in range(ROUND):
                 input_term(r, a)
                 flip_weights(1, 2 * r + a)
-                if r > 0:
-                    recurrent_term()
+            if r == 0:
+                for s in range(2 * HEAD_ROUNDS, HEAD_STATES):
+                    flip_state(s)
+                    collect_state(s)
             squash_gates(r, 0, ROUND)
             cell_products(r, 0, ROUND, nc.gpsimd)
             cell_sum(r, 0, ROUND, nc.gpsimd)
         quantise_weights(1)
+        for _ in range(2):
+            recurrent_term()
 
         def recurrent_terms(due):
             if len(terms_done) < due:
@@ -427,39 +430,42 @@ def tile_dependency_pa_t_kernel(
                     load_state(h0_rows, h0, 22, TILES)
                 if i == 4:
                     load_state(c0_rows, c0, 20, TILES)
-            early, late = ((2,), (3,)) if i < HEAD_ROUNDS else ((0, 1), (2,))
             if 1 <= i <= HEAD_ROUNDS:
                 squash_gates(i - 1, ROUND, BLOCKS)
-                new_cell(i - 1, ROUND, BLOCKS, nc.gpsimd)
+                cell_products(i - 1, ROUND, BLOCKS, nc.gpsimd)
+                cell_sum(i - 1, ROUND, BLOCKS, nc.gpsimd)
             elif i > HEAD_ROUNDS:
                 turned_sum(i - 1)
                 squash_turned(i - 1)
                 squash_gates(i - 1, 0, TURNED)
-                new_cell(i - 1, 0, BLOCKS, nc.gpsimd)
+                cell_products(i - 1, 0, BLOCKS, nc.gpsimd)
+                cell_sum(i - 1, 0, ROUND if i - 1 < SPLIT_ROUNDS else BLOCKS, nc.gpsimd)
+            needed = max(terms[min(len(terms_done) + 5, len(terms) - 1)][0], min(i + 2, last))
+            more_states = states <= needed
+            if more_states:
+                flip_state(states)
             if i >= 2:
                 squash_cell(i - 2, 0, BLOCKS)
             if i >= LAG:
                 new_hidden(i - LAG, 0, BLOCKS)
-            for b in early:
-                input_term(i, b)
             recurrent_terms(due)
-            needed = max(terms[min(len(terms_done) + 5, len(terms) - 1)][0], min(i + 2, last))
-            if states <= needed:
-                flip_state(states)
+            if more_states:
                 collect_state(states)
                 states += 1
+            for a in range(ROUND):
+                if i + 2 < ROUNDS:
+                    flip_features(i + 2, a)
+                recurrent_terms(due)
             if i + 2 < ROUNDS:
                 for a in range(ROUND):
-                    flip_features(i + 2, a)
-                collect_features(i + 2, 0)
-            recurrent_terms(due)
-            if i + 2 < ROUNDS:
-                collect_features(i + 2, 1)
-            for b in late:
+                    collect_features(i + 2, a)
+            for b in range(ROUND, BLOCKS) if i < HEAD_ROUNDS else range(TURNED):
                 input_term(i, b)
-            recurrent_terms(due)
             if i + 1 >= HEAD_ROUNDS:
                 turned_products(i + 1)
+            recurrent_terms(due)
+            if HEAD_ROUNDS <= i - 1 < SPLIT_ROUNDS:
+                cell_sum(i - 1, ROUND, BLOCKS, nc.vector)
             if i + 2 < ROUNDS:
                 quantise_features(i + 2)
 

@@ -30,6 +30,7 @@ HEAD_ROUNDS = 2
 STREAM_LOADS = 6
 LOADS_AHEAD = 5
 LAG = 3
+GATE_ORDER = (0, 1, 3, 2)
 HEAD_STATES = 5
 SPLIT_ROUNDS = 13
 WARM_MATMULS = 6
@@ -37,13 +38,15 @@ WARM_MATMULS = 6
 FLOPS = 2 * S * (IN0 + H) * DIRS * GATES
 
 
+def by_half(row_words):
+    return row_words.rearrange("r (g p u) -> r g u p", g=PASSES, u=HALVES)
+
+
 def flip_words(nc, banks, row_words, identity):
-    pass_words = HALVES * P
     bank = banks.tile([P, PASSES, HALVES, P], F32)
     for g in range(PASSES):
         for u in range(HALVES):
-            words = slice(g * pass_words + u, (g + 1) * pass_words, HALVES)
-            nc.tensor.transpose(bank[:, g, u, :], row_words[:, words], identity)
+            nc.tensor.transpose(bank[:, g, u, :], row_words[:, g, u, :], identity)
     return bank[:].rearrange("p g u r -> p g r u")
 
 
@@ -64,7 +67,8 @@ def tile_dependency_pa_t_kernel(
         stage = ctx.enter_context(tc.tile_pool(name="stage", bufs=4))
         stream = ctx.enter_context(tc.tile_pool(name="stream", bufs=STREAM_LOADS))
         state_pool = ctx.enter_context(tc.tile_pool(name="state_pool", bufs=8))
-        gate_pool = ctx.enter_context(tc.tile_pool(name="gate_pool", bufs=7))
+        gate_pool = ctx.enter_context(tc.tile_pool(name="gate_pool", bufs=8))
+        grouped_pool = ctx.enter_context(tc.tile_pool(name="grouped_pool", bufs=2))
         banks = ctx.enter_context(tc.psum_pool(name="banks", bufs=8))
 
         identity_bf16 = keep.tile([P, P], BF16)
@@ -147,7 +151,6 @@ def tile_dependency_pa_t_kernel(
         grouped_of = {}
         operand_of = {}
         gates_of = {}
-        out_gate_of = {}
         cell_of = {}
         cell_tanh_of = {}
         hidden_of = {}
@@ -162,11 +165,13 @@ def tile_dependency_pa_t_kernel(
         def prepare_small_weights(d):
             bank = banks.tile([P, 4, P], BF16)
             for r in range(4):
-                nc.tensor.transpose(bank[:, r, :], whh_rows[:, d, r, :], identity_bf16[:])
+                nc.tensor.transpose(bank[:, GATE_ORDER[r], :], whh_rows[:, d, r, :], identity_bf16[:])
             nc.scalar.copy(out=whh_t[:, d], in_=bank[:])
             bank = banks.tile([P, GATES], F32)
             nc.tensor.matmul(out=bank[:], lhsT=ones[:, 0:P], rhs=bias_rows[:, d, :], start=True, stop=True)
-            nc.scalar.copy(out=bias[:, d, :], in_=bank[:])
+            for q in range(4):
+                columns = slice(GATE_ORDER[q] * P, (GATE_ORDER[q] + 1) * P)
+                nc.scalar.copy(out=bias[:, d, columns], in_=bank[:, q * P : (q + 1) * P])
 
         def prepare_bias_column():
             bank = banks.tile([P, 4, P], F32)
@@ -175,23 +180,34 @@ def tile_dependency_pa_t_kernel(
             nc.scalar.copy(out=bias_column[:], in_=bank[:, :, 0])
 
         wih_grouped_of = {}
+        wih_sorted_of = {}
+
+        def sort_weights(d, q):
+            if d not in wih_sorted_of:
+                wih_sorted = keep.tile([P, 4, PASSES, HALVES, P], F32)
+                wih_sorted_of[d] = wih_sorted
+            nc.vector.tensor_copy(out=wih_sorted_of[d][:, q], in_=by_half(wih_words[:, d, q, :]))
 
         def flip_weights(d, q):
-            if q == 0:
-                wih_grouped = keep.tile([P, PASSES * GATES * PACK], BF16, align_bytes=64)
-                wih_grouped_of[d] = wih_grouped
-            wih_grouped_words = wih_grouped_of[d][:].bitcast(F32).rearrange(
+            half, place = divmod(GATE_ORDER[q], 2)
+            if (d, half) not in wih_grouped_of:
+                wih_grouped = grouped_pool.tile([P, PASSES * GATES // 2 * PACK], BF16, align_bytes=64)
+                wih_grouped_of[d, half] = wih_grouped
+            wih_grouped_words = wih_grouped_of[d, half][:].bitcast(F32).rearrange(
                 "p (g n u) -> p g n u", g=PASSES, u=HALVES
             )
-            flipped = flip_words(nc, banks, wih_words[:, d, q, :], identity_f32[:])
-            nc.scalar.copy(out=wih_grouped_words[:, :, q * P : (q + 1) * P, :], in_=flipped)
+            words = wih_sorted_of[d][:, q] if d in wih_sorted_of else by_half(wih_words[:, d, q, :])
+            flipped = flip_words(nc, banks, words, identity_f32[:])
+            nc.scalar.copy(out=wih_grouped_words[:, :, place * P : (place + 1) * P, :], in_=flipped)
 
-        def quantise_weights(d):
+        def quantise_weights(d, half):
+            width = GATES // 2
+            columns = slice(half * width, (half + 1) * width)
             for g in range(PASSES):
                 nc.vector.quantize_mx(
-                    out=wih_codes[:, g, d, :].bitcast(FP8X4),
-                    scales=wih_scales[:, g, d, :],
-                    in_=wih_grouped_of[d][:].rearrange("p (g c) -> p g c", g=PASSES)[:, g, :],
+                    out=wih_codes[:, g, d, columns].bitcast(FP8X4),
+                    scales=wih_scales[:, g, d, columns],
+                    in_=wih_grouped_of[d, half][:].rearrange("p (g c) -> p g c", g=PASSES)[:, g, :],
                 )
 
         def flip_state(r):
@@ -209,7 +225,7 @@ def tile_dependency_pa_t_kernel(
             h0_t_of[r] = h0_t
 
         def flip_features(r, a):
-            flipped_of[r, a] = flip_words(nc, banks, gt_of[r][:, a, :], identity_f32[:])
+            flipped_of[r, a] = flip_words(nc, banks, by_half(gt_of[r][:, a, :]), identity_f32[:])
 
         def collect_features(r, a):
             if a == 0:
@@ -313,12 +329,8 @@ def tile_dependency_pa_t_kernel(
 
         def squash(r, part, source):
             gates = gates_of[r][:, part]
-            if r not in out_gate_of:
-                out_gate = stage.tile([P, BLOCKS, H], F32)
-                out_gate_of[r] = out_gate
-            nc.scalar.activation(out=gates[:, :, 0 : 2 * H], in_=source[:, :, 0 : 2 * H], func=ACT.Sigmoid)
-            nc.scalar.activation(out=gates[:, :, 2 * H : 3 * H], in_=source[:, :, 2 * H : 3 * H], func=ACT.Tanh)
-            nc.scalar.activation(out=out_gate_of[r][:, part], in_=source[:, :, 3 * H : 4 * H], func=ACT.Sigmoid)
+            nc.scalar.activation(out=gates[:, :, 0 : 3 * H], in_=source[:, :, 0 : 3 * H], func=ACT.Sigmoid)
+            nc.scalar.activation(out=gates[:, :, 3 * H : 4 * H], in_=source[:, :, 3 * H : 4 * H], func=ACT.Tanh)
 
         def squash_gates(r, first, last):
             squash(r, slice(first, last), gates_of[r][:, first:last])
@@ -344,7 +356,7 @@ def tile_dependency_pa_t_kernel(
                 op=ALU.mult,
             )
             engine.tensor_tensor(
-                out=written[:, part], in0=gates[:, :, 0:H], in1=gates[:, :, 2 * H : 3 * H], op=ALU.mult
+                out=written[:, part], in0=gates[:, :, 0:H], in1=gates[:, :, 3 * H : 4 * H], op=ALU.mult
             )
 
         def cell_sum(r, first, last, engine):
@@ -366,7 +378,7 @@ def tile_dependency_pa_t_kernel(
             rows = hidden_of[r][:, :, dirs]
             nc.vector.tensor_tensor(
                 out=rows.rearrange("p a d h -> p d a h"),
-                in0=out_gate_of[r][:, first:last].rearrange("p (d a) h -> p d a h", a=ROUND),
+                in0=gates_of[r][:, first:last, 2 * H : 3 * H].rearrange("p (d a) h -> p d a h", a=ROUND),
                 in1=cell_tanh_of[r][:, first:last].rearrange("p (d a) h -> p d a h", a=ROUND),
                 op=ALU.mult,
             )
@@ -382,15 +394,18 @@ def tile_dependency_pa_t_kernel(
             flip_state(r)
             collect_state(r)
         prepare_small_weights(1)
-        for _ in range(BLOCKS):
+        for _ in range(BLOCKS - 1):
             recurrent_term()
         for q in range(4):
             flip_weights(0, q)
             recurrent_term()
-        quantise_weights(0)
+        for half in range(2):
+            quantise_weights(0, half)
         for r in range(HEAD_ROUNDS, 2 * HEAD_ROUNDS):
             flip_state(r)
             collect_state(r)
+            if r == HEAD_ROUNDS:
+                recurrent_term()
         prepare_bias_column()
         for r in range(HEAD_ROUNDS):
             for a in range(ROUND):
@@ -400,20 +415,21 @@ def tile_dependency_pa_t_kernel(
                 if (r, a) == (0, 0):
                     warm_up()
             quantise_features(r)
+            for a in range(ROUND):
+                sort_weights(1, ROUND * r + a)
         for r in range(HEAD_ROUNDS):
             for a in range(ROUND):
                 input_term(r, a)
-                flip_weights(1, 2 * r + a)
+                flip_weights(1, ROUND * r + a)
             if r == 0:
                 for s in range(2 * HEAD_ROUNDS, HEAD_STATES):
                     flip_state(s)
                     collect_state(s)
+            quantise_weights(1, r)
+        for r in range(HEAD_ROUNDS):
             squash_gates(r, 0, ROUND)
             cell_products(r, 0, ROUND, nc.gpsimd)
             cell_sum(r, 0, ROUND, nc.gpsimd)
-        quantise_weights(1)
-        for _ in range(2):
-            recurrent_term()
 
         def recurrent_terms(due):
             if len(terms_done) < due:
@@ -442,20 +458,20 @@ def tile_dependency_pa_t_kernel(
                 cell_sum(i - 1, 0, ROUND if i - 1 < SPLIT_ROUNDS else BLOCKS, nc.gpsimd)
             needed = max(terms[min(len(terms_done) + 5, len(terms) - 1)][0], min(i + 2, last))
             more_states = states <= needed
-            if more_states:
-                flip_state(states)
-            if i >= 2:
-                squash_cell(i - 2, 0, BLOCKS)
             if i >= LAG:
                 new_hidden(i - LAG, 0, BLOCKS)
-            recurrent_terms(due)
+            for _ in range(ROUND):
+                recurrent_terms(due)
             if more_states:
+                flip_state(states)
                 collect_state(states)
                 states += 1
+            if i >= 2:
+                squash_cell(i - 2, 0, BLOCKS)
             for a in range(ROUND):
                 if i + 2 < ROUNDS:
                     flip_features(i + 2, a)
-                recurrent_terms(due)
+            recurrent_terms(due)
             if i + 2 < ROUNDS:
                 for a in range(ROUND):
                     collect_features(i + 2, a)
@@ -464,33 +480,34 @@ def tile_dependency_pa_t_kernel(
             if i + 1 >= HEAD_ROUNDS:
                 turned_products(i + 1)
             recurrent_terms(due)
-            if HEAD_ROUNDS <= i - 1 < SPLIT_ROUNDS:
-                cell_sum(i - 1, ROUND, BLOCKS, nc.vector)
             if i + 2 < ROUNDS:
                 quantise_features(i + 2)
+            if HEAD_ROUNDS <= i - 1 < SPLIT_ROUNDS:
+                cell_sum(i - 1, ROUND, BLOCKS, nc.vector)
 
+        input_term(last, 0)
         turned_sum(last - 1)
+        turned_sum(last)
         squash_turned(last - 1)
         squash_gates(last - 1, 0, TURNED)
-        turned_sum(last)
+        new_hidden(last - 3, 0, BLOCKS)
         squash_turned(last)
-        for b in range(ROUND):
-            input_term(last, b)
-        squash_gates(last, 0, ROUND)
+        input_term(last, 1)
         squash_cell(last - 2, 0, BLOCKS)
         for b in range(ROUND, TURNED):
             input_term(last, b)
+        squash_gates(last, 0, ROUND)
         squash_gates(last, ROUND, TURNED)
-        new_hidden(last - 3, 0, BLOCKS)
         cell_products(last - 1, 0, BLOCKS, nc.vector)
         new_hidden(last - 2, 0, BLOCKS)
         cell_sum(last - 1, 0, BLOCKS, nc.vector)
+        cell_products(last, 0, ROUND, nc.vector)
         squash_cell(last - 1, 0, BLOCKS)
-        for d in range(DIRS):
-            cell_products(last, d * ROUND, (d + 1) * ROUND, nc.vector)
-        for d in range(DIRS):
-            cell_sum(last, d * ROUND, (d + 1) * ROUND, nc.vector)
-            squash_cell(last, d * ROUND, (d + 1) * ROUND)
+        cell_products(last, ROUND, BLOCKS, nc.vector)
+        cell_sum(last, 0, ROUND, nc.vector)
+        squash_cell(last, 0, ROUND)
         new_hidden(last - 1, 0, BLOCKS)
+        cell_sum(last, ROUND, BLOCKS, nc.vector)
+        squash_cell(last, ROUND, BLOCKS)
         for d in range(DIRS):
             new_hidden(last, d * ROUND, (d + 1) * ROUND)

from contextlib import ExitStack

import concourse.mybir as mybir
from concourse.masks import make_identity

F32 = mybir.dt.float32
BF16 = mybir.dt.bfloat16
U32 = mybir.dt.uint32
U8 = mybir.dt.uint8
FP8X4 = mybir.dt.float8_e4m3fn_x4
ACT = mybir.ActivationFunctionType
ALU = mybir.AluOpType

P = 128
S = 4096
H = 128
IN0 = 1024
DIRS = 2
GATES = 4 * H
PACK = 4
PAIR = 2
HALVES = PACK // PAIR
PASSES = IN0 // (P * PACK)
TILES = S // P
ROUND = 2
ROUNDS = TILES // ROUND
BLOCKS = DIRS * ROUND
TURNED = BLOCKS - 1
HEAD_ROUNDS = 2
STREAM_LOADS = 6
LOADS_AHEAD = 5
LAG = 3
GATE_ORDER = (0, 1, 3, 2)
HEAD_STATES = 5
SPLIT_ROUNDS = 13
WARM_MATMULS = 6

FLOPS = 2 * S * (IN0 + H) * DIRS * GATES


def by_half(row_words):
    return row_words.rearrange("r (g p u) -> r g u p", g=PASSES, u=HALVES)


def flip_words(nc, banks, row_words, identity):
    bank = banks.tile([P, PASSES, HALVES, P], F32)
    for g in range(PASSES):
        for u in range(HALVES):
            nc.tensor.transpose(bank[:, g, u, :], row_words[:, g, u, :], identity)
    return bank[:].rearrange("p g u r -> p g r u")


def tile_dependency_pa_t_kernel(
    tc, hn_chunks, hn_tags, x, tags, chunks, h0, c0,
    wih_f, whh_f, bih_f, bhh_f, wih_b, whh_b, bih_b, bhh_b, out,
):
    nc = tc.nc
    wih = [wih_f, wih_b]
    whh = [whh_f, whh_b]
    bih = [bih_f, bih_b]
    bhh = [bhh_f, bhh_b]

    with ExitStack() as ctx:
        ctx.enter_context(tc.manual_schedule())
        keep = ctx.enter_context(tc.tile_pool(name="keep", bufs=1))
        double = ctx.enter_context(tc.tile_pool(name="double", bufs=2))
        stage = ctx.enter_context(tc.tile_pool(name="stage", bufs=4))
        stream = ctx.enter_context(tc.tile_pool(name="stream", bufs=STREAM_LOADS))
        state_pool = ctx.enter_context(tc.tile_pool(name="state_pool", bufs=8))
        gate_pool = ctx.enter_context(tc.tile_pool(name="gate_pool", bufs=8))
        grouped_pool = ctx.enter_context(tc.tile_pool(name="grouped_pool", bufs=2))
        banks = ctx.enter_context(tc.psum_pool(name="banks", bufs=8))

        identity_bf16 = keep.tile([P, P], BF16)
        make_identity(nc, identity_bf16[:])
        identity_f32 = keep.tile([P, P], F32)
        make_identity(nc, identity_f32[:])
        ones = keep.tile([P, GATES], BF16)
        nc.vector.memset(ones[:], 1.0)
        bias_rows = keep.tile([P, DIRS, GATES], BF16)
        nc.vector.memset(bias_rows[:], 0.0)
        warm = keep.tile([P, 1], F32)
        nc.vector.memset(warm[:], 0.0)
        nc.scalar.activation(out=warm[:], in_=warm[:], func=ACT.Sigmoid)

        whh_rows = keep.tile([P, DIRS, 4, H], BF16)
        wih_rows = keep.tile([P, DIRS * 4 * IN0], BF16)
        h0_rows = keep.tile([P, DIRS, TILES, H], BF16)
        c0_rows = keep.tile([P, DIRS, TILES, H], BF16)

        wih_features = wih_rows[:].rearrange("p (d r k) -> p d r k", d=DIRS, k=IN0)
        wih_words = wih_rows[:].bitcast(F32).rearrange("p (d r w) -> p d r w", d=DIRS, w=IN0 // PAIR)

        def load_weights(d):
            for rows in (slice(0, 2), slice(2, 4)):
                nc.sync.dma_start(
                    out=wih_features[:, d, rows, :],
                    in_=wih[d].rearrange("(r p) k -> p r k", p=P)[:, rows, :],
                )

        def load_state(rows, state, first, last):
            nc.sync.dma_start(
                out=rows[:, :, first:last, :],
                in_=state.rearrange("d (p t) h -> p d t h", t=TILES)[:, :, first:last, :],
            )

        gt_of = {}

        def load_features(r):
            gt = stream.tile([P, ROUND * IN0], BF16)
            gt_features = gt[:].rearrange("p (a k) -> p a k", k=IN0)
            tiles = slice(r * ROUND, (r + 1) * ROUND)
            first = 0
            for features in (hn_chunks, hn_tags, x, tags, chunks):
                width = features.shape[1]
                nc.sync.dma_start(
                    out=gt_features[:, :, first : first + width],
                    in_=features.rearrange("(p t) c -> p t c", t=TILES)[:, tiles, :],
                )
                first += width
            gt_of[r] = gt[:].bitcast(F32).rearrange("p (a w) -> p a w", w=IN0 // PAIR)

        def load_small_weights(d):
            nc.sync.dma_start(out=whh_rows[:, d], in_=whh[d].rearrange("(r p) h -> p r h", p=P))
            nc.sync.dma_start(out=bias_rows[0:1, d, :], in_=bih[d].rearrange("(o n) -> o n", o=1))
            nc.sync.dma_start(out=bias_rows[1:2, d, :], in_=bhh[d].rearrange("(o n) -> o n", o=1))

        load_small_weights(0)
        load_state(h0_rows, h0, 0, 4)
        load_small_weights(1)
        load_weights(0)
        load_state(h0_rows, h0, 4, 12)
        load_features(0)
        load_features(1)
        load_weights(1)
        load_state(c0_rows, c0, 0, 8)
        load_features(2)
        load_state(h0_rows, h0, 12, 22)
        for r in range(3, LOADS_AHEAD):
            load_features(r)
        load_state(c0_rows, c0, 8, 20)

        whh_t = keep.tile([P, DIRS, 4, H], BF16)
        bias = keep.tile([P, DIRS, GATES], F32)
        bias_column = keep.tile([P, 4], F32)
        wih_codes = keep.tile([P, PASSES, DIRS, GATES], U32, align_bytes=64)
        wih_scales = keep.tile([P, PASSES, DIRS, GATES], U8, align_bytes=64)
        state_bank_of = {}
        flipped_of = {}
        h0_t_of = {}
        grouped_of = {}
        operand_of = {}
        gates_of = {}
        cell_of = {}
        cell_tanh_of = {}
        hidden_of = {}
        terms_done = []
        turned_of = {}
        turned_bank_of = {}

        def warm_up():
            bank = banks.tile([P, GATES], F32)
            nc.tensor.matmul(out=bank[:], lhsT=ones[:, 0:P], rhs=ones[:], start=True, stop=True)

        def prepare_small_weights(d):
            bank = banks.tile([P, 4, P], BF16)
            for r in range(4):
                nc.tensor.transpose(bank[:, GATE_ORDER[r], :], whh_rows[:, d, r, :], identity_bf16[:])
            nc.scalar.copy(out=whh_t[:, d], in_=bank[:])
            bank = banks.tile([P, GATES], F32)
            nc.tensor.matmul(out=bank[:], lhsT=ones[:, 0:P], rhs=bias_rows[:, d, :], start=True, stop=True)
            for q in range(4):
                columns = slice(GATE_ORDER[q] * P, (GATE_ORDER[q] + 1) * P)
                nc.scalar.copy(out=bias[:, d, columns], in_=bank[:, q * P : (q + 1) * P])

        def prepare_bias_column():
            bank = banks.tile([P, 4, P], F32)
            for q in range(4):
                nc.tensor.transpose(bank[:, q, :], bias[:, 1, q * P : (q + 1) * P], identity_f32[:])
            nc.scalar.copy(out=bias_column[:], in_=bank[:, :, 0])

        wih_grouped_of = {}
        wih_sorted_of = {}

        def sort_weights(d, q):
            if d not in wih_sorted_of:
                wih_sorted = keep.tile([P, 4, PASSES, HALVES, P], F32)
                wih_sorted_of[d] = wih_sorted
            nc.vector.tensor_copy(out=wih_sorted_of[d][:, q], in_=by_half(wih_words[:, d, q, :]))

        def flip_weights(d, q):
            half, place = divmod(GATE_ORDER[q], 2)
            if (d, half) not in wih_grouped_of:
                wih_grouped = grouped_pool.tile([P, PASSES * GATES // 2 * PACK], BF16, align_bytes=64)
                wih_grouped_of[d, half] = wih_grouped
            wih_grouped_words = wih_grouped_of[d, half][:].bitcast(F32).rearrange(
                "p (g n u) -> p g n u", g=PASSES, u=HALVES
            )
            words = wih_sorted_of[d][:, q] if d in wih_sorted_of else by_half(wih_words[:, d, q, :])
            flipped = flip_words(nc, banks, words, identity_f32[:])
            nc.scalar.copy(out=wih_grouped_words[:, :, place * P : (place + 1) * P, :], in_=flipped)

        def quantise_weights(d, half):
            width = GATES // 2
            columns = slice(half * width, (half + 1) * width)
            for g in range(PASSES):
                nc.vector.quantize_mx(
                    out=wih_codes[:, g, d, columns].bitcast(FP8X4),
                    scales=wih_scales[:, g, d, columns],
                    in_=wih_grouped_of[d, half][:].rearrange("p (g c) -> p g c", g=PASSES)[:, g, :],
                )

        def flip_state(r):
            bank = banks.tile([P, DIRS, ROUND, P], BF16)
            for d in range(DIRS):
                for a in range(ROUND):
                    nc.tensor.transpose(
                        bank[:, d, a, :], h0_rows[:, d, r * ROUND + a, :], identity_bf16[:]
                    )
            state_bank_of[r] = bank

        def collect_state(r):
            h0_t = state_pool.tile([P, DIRS, ROUND, P], BF16)
            nc.scalar.copy(out=h0_t[:], in_=state_bank_of[r][:])
            h0_t_of[r] = h0_t

        def flip_features(r, a):
            flipped_of[r, a] = flip_words(nc, banks, by_half(gt_of[r][:, a, :]), identity_f32[:])

        def collect_features(r, a):
            if a == 0:
                grouped = double.tile([P, ROUND * PASSES * P * PACK], BF16, align_bytes=64)
                grouped_of[r] = grouped
            grouped_words = grouped_of[r][:].bitcast(F32).rearrange(
                "p (a g r u) -> p a g r u", a=ROUND, g=PASSES, u=HALVES
            )
            nc.scalar.copy(out=grouped_words[:, a], in_=flipped_of[r, a])

        def quantise_features(r):
            codes = stage.tile([P, ROUND, PASSES, P], U32, align_bytes=64)
            scales = stage.tile([P, ROUND, PASSES, P], U8, align_bytes=64)
            nc.vector.quantize_mx(
                out=codes[:].rearrange("p a g r -> p (a g r)").bitcast(FP8X4),
                scales=scales[:].rearrange("p a g r -> p (a g r)"),
                in_=grouped_of[r][:],
            )
            operand_of[r] = (codes, scales)

        blocks = [(d, a) for d in range(DIRS) for a in range(ROUND)]
        terms = [(r, b) for d in range(DIRS) for r in range(HEAD_ROUNDS) for b in (2 * d, 2 * d + 1)]
        terms += [(r, b) for r in range(HEAD_ROUNDS, ROUNDS) for b in range(TURNED)]

        def recurrent_product(r, b, stop):
            d, a = blocks[b]
            bank = banks.tile([P, GATES], F32)
            nc.tensor.matmul(
                out=bank[:],
                lhsT=h0_t_of[r][:, d, a, :],
                rhs=whh_t[:, d].rearrange("p r h -> p (r h)"),
                start=True,
                stop=stop,
            )
            return bank

        def recurrent_term():
            r, b = terms[len(terms_done)]
            terms_done.append((r, b))
            if r not in gates_of:
                gates = gate_pool.tile([P, BLOCKS, GATES], F32)
                gates_of[r] = gates
            bank = recurrent_product(r, b, True)
            nc.vector.tensor_tensor(
                out=gates_of[r][:, b, :], in0=bank[:], in1=bias[:, b // ROUND, :], op=ALU.add
            )

        def input_term(r, b):
            d, a = blocks[b]
            codes, scales = operand_of[r]
            bank = banks.tile([P, GATES], F32)
            for g in range(PASSES):
                nc.tensor.matmul_mx(
                    out=bank[:],
                    lhsT=codes[:, a, g, :].bitcast(FP8X4),
                    lhsT_scale=scales[:, a, g, :],
                    rhs=wih_codes[:, g, d, :].bitcast(FP8X4),
                    rhs_scale=wih_scales[:, g, d, :],
                    start=(g == 0),
                    stop=(g == PASSES - 1),
                )
            nc.vector.tensor_tensor(
                out=gates_of[r][:, b, :], in0=bank[:], in1=gates_of[r][:, b, :], op=ALU.add
            )

        def turned_products(r):
            a = TURNED % ROUND
            codes, scales = operand_of[r]
            bank = banks.tile([P, 4, P], F32)
            for q in range(4):
                columns = slice(q * P, (q + 1) * P)
                for g in range(PASSES):
                    nc.tensor.matmul_mx(
                        out=bank[:, q, :],
                        lhsT=wih_codes[:, g, TURNED // ROUND, columns].bitcast(FP8X4),
                        lhsT_scale=wih_scales[:, g, TURNED // ROUND, columns],
                        rhs=codes[:, a, g, :].bitcast(FP8X4),
                        rhs_scale=scales[:, a, g, :],
                        start=(g == 0),
                        stop=(g == PASSES - 1),
                    )
            turned = double.tile([P, 4, P], F32)
            for q in range(4):
                nc.scalar.activation(
                    out=turned[:, q, :], in_=bank[:, q, :], func=ACT.Identity, bias=bias_column[:, q : q + 1]
                )
            turned_of[r] = turned

        def turned_sum(r):
            bank = recurrent_product(r, TURNED, False)
            for q in range(4):
                nc.tensor.matmul(
                    out=bank[:, q * P : (q + 1) * P],
                    lhsT=turned_of[r][:, q, :],
                    rhs=identity_f32[:],
                    start=False,
                    stop=(q == 3),
                    is_transpose=True,
                )
            turned_bank_of[r] = bank

        def squash(r, part, source):
            gates = gates_of[r][:, part]
            nc.scalar.activation(out=gates[:, :, 0 : 3 * H], in_=source[:, :, 0 : 3 * H], func=ACT.Sigmoid)
            nc.scalar.activation(out=gates[:, :, 3 * H : 4 * H], in_=source[:, :, 3 * H : 4 * H], func=ACT.Tanh)

        def squash_gates(r, first, last):
            squash(r, slice(first, last), gates_of[r][:, first:last])

        def squash_turned(r):
            squash(r, slice(TURNED, TURNED + 1), turned_bank_of[r][:].rearrange("p (b n) -> p b n", b=1))

        def cell_products(r, first, last, engine):
            part = slice(first, last)
            gates = gates_of[r][:, part]
            tiles = slice(r * ROUND, (r + 1) * ROUND)
            dirs = slice(first // ROUND, (last + ROUND - 1) // ROUND)
            if r not in cell_of:
                kept = double.tile([P, BLOCKS, H], F32)
                written = double.tile([P, BLOCKS, H], F32)
                cell = stage.tile([P, BLOCKS, H], F32)
                cell_of[r] = (kept, written, cell)
            kept, written, cell = cell_of[r]
            engine.tensor_tensor(
                out=kept[:, part].rearrange("p (d a) h -> p d a h", a=ROUND),
                in0=gates[:, :, H : 2 * H].rearrange("p (d a) h -> p d a h", a=ROUND),
                in1=c0_rows[:, dirs, tiles, :],
                op=ALU.mult,
            )
            engine.tensor_tensor(
                out=written[:, part], in0=gates[:, :, 0:H], in1=gates[:, :, 3 * H : 4 * H], op=ALU.mult
            )

        def cell_sum(r, first, last, engine):
            kept, written, cell = cell_of[r]
            engine.tensor_tensor(out=cell[:, first:last], in0=kept[:, first:last], in1=written[:, first:last], op=ALU.add)

        def squash_cell(r, first, last):
            if r not in cell_tanh_of:
                cell_tanh = double.tile([P, BLOCKS, H], F32)
                cell_tanh_of[r] = cell_tanh
            nc.scalar.activation(out=cell_tanh_of[r][:, first:last], in_=cell_of[r][2][:, first:last], func=ACT.Tanh)

        def new_hidden(r, first, last):
            tiles = slice(r * ROUND, (r + 1) * ROUND)
            dirs = slice(first // ROUND, (last + ROUND - 1) // ROUND)
            if r not in hidden_of:
                hidden = stage.tile([P, ROUND, DIRS, H], F32)
                hidden_of[r] = hidden
            rows = hidden_of[r][:, :, dirs]
            nc.vector.tensor_tensor(
                out=rows.rearrange("p a d h -> p d a h"),
                in0=gates_of[r][:, first:last, 2 * H : 3 * H].rearrange("p (d a) h -> p d a h", a=ROUND),
                in1=cell_tanh_of[r][:, first:last].rearrange("p (d a) h -> p d a h", a=ROUND),
                op=ALU.mult,
            )
            nc.sync.dma_start(
                out=out.rearrange("(p t) (d h) -> p t d h", t=TILES, d=DIRS)[:, tiles, dirs, :], in_=rows
            )

        for _ in range(WARM_MATMULS):
            warm_up()
        prepare_small_weights(0)
        warm_up()
        for r in range(HEAD_ROUNDS):
            flip_state(r)
            collect_state(r)
        prepare_small_weights(1)
        for _ in range(BLOCKS - 1):
            recurrent_term()
        for q in range(4):
            flip_weights(0, q)
            recurrent_term()
        for half in range(2):
            quantise_weights(0, half)
        for r in range(HEAD_ROUNDS, 2 * HEAD_ROUNDS):
            flip_state(r)
            collect_state(r)
            if r == HEAD_ROUNDS:
                recurrent_term()
        prepare_bias_column()
        for r in range(HEAD_ROUNDS):
            for a in range(ROUND):
                flip_features(r, a)
                collect_features(r, a)
                recurrent_term()
                if (r, a) == (0, 0):
                    warm_up()
            quantise_features(r)
            for a in range(ROUND):
                sort_weights(1, ROUND * r + a)
        for r in range(HEAD_ROUNDS):
            for a in range(ROUND):
                input_term(r, a)
                flip_weights(1, ROUND * r + a)
            if r == 0:
                for s in range(2 * HEAD_ROUNDS, HEAD_STATES):
                    flip_state(s)
                    collect_state(s)
            quantise_weights(1, r)
        for r in range(HEAD_ROUNDS):
            squash_gates(r, 0, ROUND)
            cell_products(r, 0, ROUND, nc.gpsimd)
            cell_sum(r, 0, ROUND, nc.gpsimd)

        def recurrent_terms(due):
            if len(terms_done) < due:
                recurrent_term()

        states = HEAD_STATES
        last = ROUNDS - 1
        head_terms = len(terms_done)
        for i in range(last):
            due = min(len(terms), head_terms + (len(terms) - head_terms) * (i + 1) / (ROUNDS - 2))
            if i + LOADS_AHEAD < ROUNDS:
                load_features(i + LOADS_AHEAD)
                if i == 2:
                    load_state(h0_rows, h0, 22, TILES)
                if i == 4:
                    load_state(c0_rows, c0, 20, TILES)
            if 1 <= i <= HEAD_ROUNDS:
                squash_gates(i - 1, ROUND, BLOCKS)
                cell_products(i - 1, ROUND, BLOCKS, nc.gpsimd)
                cell_sum(i - 1, ROUND, BLOCKS, nc.gpsimd)
            elif i > HEAD_ROUNDS:
                turned_sum(i - 1)
                squash_turned(i - 1)
                squash_gates(i - 1, 0, TURNED)
                cell_products(i - 1, 0, BLOCKS, nc.gpsimd)
                cell_sum(i - 1, 0, ROUND if i - 1 < SPLIT_ROUNDS else BLOCKS, nc.gpsimd)
            needed = max(terms[min(len(terms_done) + 5, len(terms) - 1)][0], min(i + 2, last))
            more_states = states <= needed
            if i >= LAG:
                new_hidden(i - LAG, 0, BLOCKS)
            for _ in range(ROUND):
                recurrent_terms(due)
            if more_states:
                flip_state(states)
                collect_state(states)
                states += 1
            if i >= 2:
                squash_cell(i - 2, 0, BLOCKS)
            for a in range(ROUND):
                if i + 2 < ROUNDS:
                    flip_features(i + 2, a)
            recurrent_terms(due)
            if i + 2 < ROUNDS:
                for a in range(ROUND):
                    collect_features(i + 2, a)
            for b in range(ROUND, BLOCKS) if i < HEAD_ROUNDS else range(TURNED):
                input_term(i, b)
            if i + 1 >= HEAD_ROUNDS:
                turned_products(i + 1)
            recurrent_terms(due)
            if i + 2 < ROUNDS:
                quantise_features(i + 2)
            if HEAD_ROUNDS <= i - 1 < SPLIT_ROUNDS:
                cell_sum(i - 1, ROUND, BLOCKS, nc.vector)

        input_term(last, 0)
        turned_sum(last - 1)
        turned_sum(last)
        squash_turned(last - 1)
        squash_gates(last - 1, 0, TURNED)
        new_hidden(last - 3, 0, BLOCKS)
        squash_turned(last)
        input_term(last, 1)
        squash_cell(last - 2, 0, BLOCKS)
        for b in range(ROUND, TURNED):
            input_term(last, b)
        squash_gates(last, 0, ROUND)
        squash_gates(last, ROUND, TURNED)
        cell_products(last - 1, 0, BLOCKS, nc.vector)
        new_hidden(last - 2, 0, BLOCKS)
        cell_sum(last - 1, 0, BLOCKS, nc.vector)
        cell_products(last, 0, ROUND, nc.vector)
        squash_cell(last - 1, 0, BLOCKS)
        cell_products(last, ROUND, BLOCKS, nc.vector)
        cell_sum(last, 0, ROUND, nc.vector)
        squash_cell(last, 0, ROUND)
        new_hidden(last - 1, 0, BLOCKS)
        cell_sum(last, ROUND, BLOCKS, nc.vector)
        squash_cell(last, ROUND, BLOCKS)
        for d in range(DIRS):
            new_hidden(last, d * ROUND, (d + 1) * ROUND)
